import numpy as np
import ml_dtypes


def mxq(x, axis, fmt="e4m3"):
    dtype, down = {"e4m3": (ml_dtypes.float8_e4m3fn, 7), "e5m2": (ml_dtypes.float8_e5m2, 14)}[fmt]
    v = np.moveaxis(np.asarray(x, np.float32).astype(ml_dtypes.bfloat16).astype(np.float64), axis, -1)
    blocks = v.reshape(v.shape[:-1] + (-1, 32))
    amax = np.abs(blocks).max(-1, keepdims=True)
    byte = np.maximum(np.where(amax > 0, np.frexp(amax)[1] - 1 + 127, 0) - down, 1)
    scale = np.exp2(byte - 127.0)
    codes = (blocks / scale).astype(np.float32).astype(dtype).astype(np.float64)
    return np.moveaxis((codes * scale).reshape(v.shape), -1, axis)


WIDE = False


def mx_kscale(k):
    if not WIDE:
        return np.ones(k)
    levels = np.array([10, -10, 5, -5, 0])
    a = np.random.permutation(np.resize(levels, k // 512 * 4)).reshape(k // 512, 4)
    idx = np.arange(k)
    return np.exp2(a[idx // 512, idx % 128 // 32])


BF16 = ml_dtypes.bfloat16


def bf(x):
    return np.asarray(x, np.float32).astype(BF16)


def f64(x):
    return np.asarray(x).astype(np.float64)


B, N, HH, WW, TC, IC, DQK = 12, 256, 32, 32, 256, 512, 512
M = HH * WW
BSIG = 2.0


def setup_inputs():
    s = mx_kscale(IC)
    z = np.random.standard_normal((B, N, M)) * BSIG
    e = np.exp(z - z.max(-1, keepdims=True))
    keep = np.random.uniform(size=(B, N, M)) > 0.2
    return {"beta": bf(e / e.sum(-1, keepdims=True) * keep),
            "x2": bf(np.random.standard_normal((B, HH, WW, IC)) * s),
            "Wv": bf(np.random.standard_normal((IC, TC)) * 2.0 / np.sqrt(IC) / s[:, None]),
            "bv": bf(np.random.standard_normal(TC) * 0.25)}


def reference(beta, x2, Wv, bv):
    v = (mxq(f64(x2).reshape(B, M, IC), 2, "e4m3") @ mxq(f64(Wv), 0, "e4m3")) + f64(bv)
    return mxq(f64(beta), 2, "e4m3") @ mxq(v, 1, "e4m3")

@@ -1,0 +1,187 @@
+from contextlib import ExitStack
+
+import concourse.bass as bass
+import concourse.masks as masks
+import concourse.mybir as mybir
+import concourse.tile as tile
+
+F32 = mybir.dt.float32
+BF16 = mybir.dt.bfloat16
+U32 = mybir.dt.uint32
+U8 = mybir.dt.uint8
+FP8X4 = mybir.dt.float8_e4m3fn_x4
+ADD = mybir.AluOpType.add
+
+P = 128
+B, NW, M, IC, TC = 12, 256, 1024, 512, 256
+STEPS = 2 * B
+FLOPS = 2 * B * M * IC * TC + 2 * B * NW * M * TC
+MANUAL = True
+
+
+def tile_text2imgca_pb_t_kernel(tc, beta, x2, Wv, bv, out):
+    nc = tc.nc
+    with ExitStack() as ctx:
+        res = ctx.enter_context(tc.tile_pool(name="res", bufs=1))
+        p3 = ctx.enter_context(tc.tile_pool(name="p3", bufs=3))
+        p6 = ctx.enter_context(tc.tile_pool(name="p6", bufs=6))
+        ps_tr = ctx.enter_context(tc.psum_pool(name="ps_tr", bufs=4))
+        ps_v = ctx.enter_context(tc.psum_pool(name="ps_v", bufs=3))
+        ps_o = ctx.enter_context(tc.psum_pool(name="ps_o", bufs=1))
+        if MANUAL:
+            ctx.enter_context(tc.manual_schedule())
+
+        x_sb = []
+        b_sb = []
+        o_sb = []
+        for b in range(B):
+            x_t = res.tile([P, 4096], BF16, name="x%d" % b)
+            b_t = res.tile([P, 2048], BF16, name="b%d" % b)
+            o_t = res.tile([P, 512], F32, name="o%d" % b)
+            x_sb.append(x_t)
+            b_sb.append(b_t)
+            o_sb.append(o_t)
+        w_raw = res.tile([P, 1024], BF16, name="w_raw")
+        w_grp = res.tile([P, 1024], BF16, name="w_grp", align_bytes=64)
+        w_codes = res.tile([P, 256], U32, name="w_codes", align_bytes=64)
+        w_scales = res.tile([P, 256], U8, name="w_scales", align_bytes=64)
+        brow = res.tile([P, TC], BF16, name="brow")
+        ones = res.tile([P, P], BF16, name="ones")
+        bias = res.tile([P, TC], F32, name="bias")
+        ident = res.tile([P, P], F32, name="ident")
+
+        def x_view(b):
+            return x2[b].rearrange("h w c -> (h w) c").rearrange("(a p e) c -> p a (e c)", a=4, p=P, e=2)
+
+        nc.vector.memset(brow[:], 0.0)
+        nc.vector.memset(ones[:], 1.0)
+        masks.make_identity(nc, ident[:])
+
+        x0 = x_sb[0][:].rearrange("p (a f) -> p a f", a=4)
+        nc.sync.dma_start(out=x0[:, 0:2, :], in_=x_view(0)[:, 0:2, :])
+        nc.sync.dma_start(
+            out=w_raw[:].rearrange("q (u f) -> q u f", u=2),
+            in_=Wv.rearrange("(u q e) n -> q u (e n)", u=2, q=P, e=2),
+        )
+        nc.sync.dma_start(out=brow[0:1, :], in_=bv.rearrange("(o n) -> o n", o=1))
+        nc.sync.dma_start(out=b_sb[0][:], in_=beta[0].rearrange("(p h) m -> p (h m)", h=2))
+        nc.sync.dma_start(out=x0[:, 2:4, :], in_=x_view(0)[:, 2:4, :])
+        for b in range(1, B):
+            nc.sync.dma_start(out=x_sb[b][:].rearrange("p (a f) -> p a f", a=4), in_=x_view(b))
+            nc.sync.dma_start(out=b_sb[b][:], in_=beta[b].rearrange("(p h) m -> p (h m)", h=2))
+
+        nc.vector.tensor_copy(
+            out=w_grp[:].rearrange("q (n t) -> q n t", t=4),
+            in_=w_raw[:].rearrange("q (t n) -> q n t", t=4),
+        )
+        nc.vector.quantize_mx(out=w_codes[:].bitcast(FP8X4), scales=w_scales[:], in_=w_grp[:])
+
+        xg = {}
+        bg = {}
+        xq = {}
+        bq = {}
+        vbank = {}
+        vg = {}
+        vq = {}
+
+        def out_of_bank(dst_bf16, bank):
+            nc.scalar.copy(
+                out=dst_bf16.bitcast(F32).rearrange("q (i m u) -> q i m u", i=2, u=2),
+                in_=bank[:].rearrange("q (i u m) -> q i m u", i=2, u=2),
+            )
+
+        def transposes(s):
+            b, g = divmod(s, 2)
+            xw = x_sb[b][:].bitcast(F32)
+            bw = b_sb[b][:].bitcast(F32)
+            xg_t = p3.tile([P, 2048], BF16, name="xg", align_bytes=64)
+            bg_t = p3.tile([P, 1024], BF16, name="bg", align_bytes=64)
+            xg[s] = xg_t
+            bg[s] = bg_t
+            for half in range(2):
+                bank = ps_tr.tile([P, 512], F32, name="tr")
+                for i in range(2):
+                    j = 4 * g + 2 * half + i
+                    for u in range(2):
+                        c0 = 256 * j + 128 * u
+                        d0 = (2 * i + u) * 128
+                        nc.tensor.transpose(bank[:, d0:d0 + 128], xw[:, c0:c0 + 128], ident[:])
+                out_of_bank(xg_t[:, 1024 * half:1024 * half + 1024], bank)
+            bank = ps_tr.tile([P, 512], F32, name="tr")
+            for h in range(2):
+                for u in range(2):
+                    c0 = 512 * h + 128 * (2 * g + u)
+                    d0 = (2 * h + u) * 128
+                    nc.tensor.transpose(bank[:, d0:d0 + 128], bw[:, c0:c0 + 128], ident[:])
+            out_of_bank(bg_t[:], bank)
+
+        def quantise(src, width, pool, label):
+            codes = pool.tile([P, width // 4], U32, name=label + "c", align_bytes=64)
+            scales = pool.tile([P, width // 4], U8, name=label + "s", align_bytes=64)
+            nc.vector.quantize_mx(out=codes[:].bitcast(FP8X4), scales=scales[:], in_=src[:])
+            return codes, scales
+
+        def first_product(s):
+            codes, scales = xq[s]
+            banks = []
+            for hf in range(2):
+                bank = ps_v.tile([P, 512], F32, name="v")
+                for t in range(4):
+                    nc.tensor.matmul_mx(
+                        out=bank[:, 128 * t:128 * t + 128],
+                        lhsT=codes[:, 128 * t:128 * t + 128].bitcast(FP8X4),
+                        lhsT_scale=scales[:, 128 * t:128 * t + 128],
+                        rhs=w_codes[:, 128 * hf:128 * hf + 128].bitcast(FP8X4),
+                        rhs_scale=w_scales[:, 128 * hf:128 * hf + 128],
+                        start=True,
+                        stop=True,
+                    )
+                banks.append(bank)
+            vbank[s] = banks
+
+        def add_bias(s):
+            vg_t = p3.tile([P, 1024], BF16, name="vg", align_bytes=64)
+            vg[s] = vg_t
+            for hf in range(2):
+                nc.vector.tensor_tensor(
+                    out=vg_t[:, 512 * hf:512 * hf + 512].rearrange("p (w t) -> p w t", t=4),
+                    in0=vbank[s][hf][:].rearrange("p (t w) -> p w t", t=4),
+                    in1=bias[:, 128 * hf:128 * hf + 128].unsqueeze(2).to_broadcast([P, 128, 4]),
+                    op=ADD,
+                )
+
+        def second_product(b):
+            bank = ps_o.tile([P, 512], F32, name="o")
+            for h in range(2):
+                for g in range(2):
+                    s = 2 * b + g
+                    nc.tensor.matmul_mx(
+                        out=bank[:, 256 * h:256 * h + 256],
+                        lhsT=bq[s][0][:, 128 * h:128 * h + 128].bitcast(FP8X4),
+                        lhsT_scale=bq[s][1][:, 128 * h:128 * h + 128],
+                        rhs=vq[s][0][:].bitcast(FP8X4),
+                        rhs_scale=vq[s][1][:],
+                        start=(g == 0),
+                        stop=(g == 1),
+                    )
+            nc.scalar.copy(out=o_sb[b][:], in_=bank[:])
+            nc.sync.dma_start(out=out[b].rearrange("(p h) n -> p (h n)", h=2), in_=o_sb[b][:])
+
+        for k in range(STEPS + 4):
+            if k < STEPS:
+                transposes(k)
+            if k == 1:
+                bank = ps_o.tile([P, 512], F32, name="o")
+                nc.tensor.matmul(out=bank[:, 0:TC], lhsT=ones[:], rhs=brow[:], start=True, stop=True)
+                nc.vector.tensor_copy(out=bias[:], in_=bank[:, 0:TC])
+            if 0 <= k - 1 < STEPS:
+                xq[k - 1] = quantise(xg[k - 1], 2048, p3, "x")
+            if 0 <= k - 2 < STEPS:
+                add_bias(k - 2)
+            if 0 <= k - 1 < STEPS:
+                first_product(k - 1)
+                bq[k - 1] = quantise(bg[k - 1], 1024, p6, "b")
+            if 0 <= k - 2 < STEPS:
+                vq[k - 2] = quantise(vg[k - 2], 1024, p6, "v")
+            if k >= 4 and k % 2 == 0:
+                second_product((k - 4) // 2)

@@ -1,9 +1,7 @@
 from contextlib import ExitStack
 
-import concourse.bass as bass
 import concourse.masks as masks
 import concourse.mybir as mybir
-import concourse.tile as tile
 
 F32 = mybir.dt.float32
 BF16 = mybir.dt.bfloat16
@@ -33,14 +31,12 @@ def tile_text2imgca_pb_t_kernel(tc, beta, x2, Wv, bv, out):
 
         x_sb = []
         b_sb = []
-        o_sb = []
-        for b in range(B):
-            x_t = res.tile([P, 4096], BF16, name="x%d" % b)
-            b_t = res.tile([P, 2048], BF16, name="b%d" % b)
-            o_t = res.tile([P, 512], F32, name="o%d" % b)
+        for s in range(STEPS):
+            x_t = res.tile([P, 2048], BF16, name="x%d" % s)
             x_sb.append(x_t)
+        for b in range(B):
+            b_t = res.tile([P, 2048], BF16, name="b%d" % b)
             b_sb.append(b_t)
-            o_sb.append(o_t)
         w_raw = res.tile([P, 1024], BF16, name="w_raw")
         w_grp = res.tile([P, 1024], BF16, name="w_grp", align_bytes=64)
         w_codes = res.tile([P, 256], U32, name="w_codes", align_bytes=64)
@@ -50,25 +46,32 @@ def tile_text2imgca_pb_t_kernel(tc, beta, x2, Wv, bv, out):
         bias = res.tile([P, TC], F32, name="bias")
         ident = res.tile([P, P], F32, name="ident")
 
-        def x_view(b):
-            return x2[b].rearrange("h w c -> (h w) c").rearrange("(a p e) c -> p a (e c)", a=4, p=P, e=2)
-
         nc.vector.memset(brow[:], 0.0)
         nc.vector.memset(ones[:], 1.0)
         masks.make_identity(nc, ident[:])
 
-        x0 = x_sb[0][:].rearrange("p (a f) -> p a f", a=4)
-        nc.sync.dma_start(out=x0[:, 0:2, :], in_=x_view(0)[:, 0:2, :])
+        def load_x(s):
+            b, g = divmod(s, 2)
+            src = x2[b].rearrange("h w c -> (h w) c").rearrange("(a p e) c -> p a (e c)", a=4, p=P, e=2)
+            nc.sync.dma_start(
+                out=x_sb[s][:].rearrange("p (a f) -> p a f", a=2), in_=src[:, 2 * g:2 * g + 2, :]
+            )
+
+        def load_beta(b):
+            nc.sync.dma_start(out=b_sb[b][:], in_=beta[b].rearrange("(p h) m -> p (h m)", h=2))
+
+        load_x(0)
         nc.sync.dma_start(
             out=w_raw[:].rearrange("q (u f) -> q u f", u=2),
             in_=Wv.rearrange("(u q e) n -> q u (e n)", u=2, q=P, e=2),
         )
         nc.sync.dma_start(out=brow[0:1, :], in_=bv.rearrange("(o n) -> o n", o=1))
-        nc.sync.dma_start(out=b_sb[0][:], in_=beta[0].rearrange("(p h) m -> p (h m)", h=2))
-        nc.sync.dma_start(out=x0[:, 2:4, :], in_=x_view(0)[:, 2:4, :])
+        load_x(1)
+        load_beta(0)
         for b in range(1, B):
-            nc.sync.dma_start(out=x_sb[b][:].rearrange("p (a f) -> p a f", a=4), in_=x_view(b))
-            nc.sync.dma_start(out=b_sb[b][:], in_=beta[b].rearrange("(p h) m -> p (h m)", h=2))
+            load_x(2 * b)
+            load_x(2 * b + 1)
+            load_beta(b)
 
         nc.vector.tensor_copy(
             out=w_grp[:].rearrange("q (n t) -> q n t", t=4),
@@ -90,23 +93,22 @@ def tile_text2imgca_pb_t_kernel(tc, beta, x2, Wv, bv, out):
                 in_=bank[:].rearrange("q (i u m) -> q i m u", i=2, u=2),
             )
 
-        def transposes(s):
-            b, g = divmod(s, 2)
-            xw = x_sb[b][:].bitcast(F32)
-            bw = b_sb[b][:].bitcast(F32)
+        def transpose_x(s):
+            xw = x_sb[s][:].bitcast(F32)
             xg_t = p3.tile([P, 2048], BF16, name="xg", align_bytes=64)
-            bg_t = p3.tile([P, 1024], BF16, name="bg", align_bytes=64)
             xg[s] = xg_t
-            bg[s] = bg_t
             for half in range(2):
                 bank = ps_tr.tile([P, 512], F32, name="tr")
-                for i in range(2):
-                    j = 4 * g + 2 * half + i
-                    for u in range(2):
-                        c0 = 256 * j + 128 * u
-                        d0 = (2 * i + u) * 128
-                        nc.tensor.transpose(bank[:, d0:d0 + 128], xw[:, c0:c0 + 128], ident[:])
+                for i in range(4):
+                    c0 = 512 * half + 128 * i
+                    nc.tensor.transpose(bank[:, 128 * i:128 * i + 128], xw[:, c0:c0 + 128], ident[:])
                 out_of_bank(xg_t[:, 1024 * half:1024 * half + 1024], bank)
+
+        def transpose_beta(s):
+            b, g = divmod(s, 2)
+            bw = b_sb[b][:].bitcast(F32)
+            bg_t = p3.tile([P, 1024], BF16, name="bg", align_bytes=64)
+            bg[s] = bg_t
             bank = ps_tr.tile([P, 512], F32, name="tr")
             for h in range(2):
                 for u in range(2):
@@ -120,6 +122,9 @@ def tile_text2imgca_pb_t_kernel(tc, beta, x2, Wv, bv, out):
             scales = pool.tile([P, width // 4], U8, name=label + "s", align_bytes=64)
             nc.vector.quantize_mx(out=codes[:].bitcast(FP8X4), scales=scales[:], in_=src[:])
             return codes, scales
+
+        def quantise_x(s):
+            xq[s] = quantise(xg[s], 2048, p3, "x")
 
         def first_product(s):
             codes, scales = xq[s]
@@ -150,38 +155,78 @@ def tile_text2imgca_pb_t_kernel(tc, beta, x2, Wv, bv, out):
                     op=ADD,
                 )
 
+        def second_pass(acc, b, g, h):
+            s = 2 * b + g
+            nc.tensor.matmul_mx(
+                out=acc,
+                lhsT=bq[s][0][:, 128 * h:128 * h + 128].bitcast(FP8X4),
+                lhsT_scale=bq[s][1][:, 128 * h:128 * h + 128],
+                rhs=vq[s][0][:].bitcast(FP8X4),
+                rhs_scale=vq[s][1][:],
+                start=(g == 0),
+                stop=(g == 1),
+            )
+
         def second_product(b):
             bank = ps_o.tile([P, 512], F32, name="o")
             for h in range(2):
                 for g in range(2):
-                    s = 2 * b + g
-                    nc.tensor.matmul_mx(
-                        out=bank[:, 256 * h:256 * h + 256],
-                        lhsT=bq[s][0][:, 128 * h:128 * h + 128].bitcast(FP8X4),
-                        lhsT_scale=bq[s][1][:, 128 * h:128 * h + 128],
-                        rhs=vq[s][0][:].bitcast(FP8X4),
-                        rhs_scale=vq[s][1][:],
-                        start=(g == 0),
-                        stop=(g == 1),
-                    )
-            nc.scalar.copy(out=o_sb[b][:], in_=bank[:])
-            nc.sync.dma_start(out=out[b].rearrange("(p h) n -> p (h n)", h=2), in_=o_sb[b][:])
+                    second_pass(bank[:, 256 * h:256 * h + 256], b, g, h)
+            o_t = p6.tile([P, 512], F32, name="o_sb")
+            nc.scalar.copy(out=o_t[:], in_=bank[:])
+            nc.sync.dma_start(out=out[b].rearrange("(p h) n -> p (h n)", h=2), in_=o_t[:])
 
-        for k in range(STEPS + 4):
-            if k < STEPS:
-                transposes(k)
-            if k == 1:
+        last = []
+
+        def last_product(g):
+            b = B - 1
+            if g == 0:
+                bank0 = ps_o.tile([P, 512], F32, name="o")
+                bank1 = ps_tr.tile([P, 512], F32, name="tr")
+                last.append(bank0)
+                last.append(bank1)
+            for h in range(2):
+                second_pass(last[h][:, 0:256], b, g, h)
+            if g == 1:
+                dst = out[b].rearrange("(p h) n -> p h n", h=2)
+                o0 = res.tile([P, 256], F32, name="o_last0")
+                o1 = res.tile([P, 256], F32, name="o_last1")
+                nc.scalar.copy(out=o0[:], in_=last[0][:, 0:256])
+                nc.sync.dma_start(out=dst[:, 0, :], in_=o0[:])
+                nc.vector.tensor_copy(out=o1[:], in_=last[1][:, 0:256])
+                nc.sync.dma_start(out=dst[:, 1, :], in_=o1[:])
+
+        def live(s):
+            return 0 <= s < STEPS
+
+        for k in range(STEPS + 3):
+            if live(k):
+                transpose_x(k)
+            if k == 0:
                 bank = ps_o.tile([P, 512], F32, name="o")
                 nc.tensor.matmul(out=bank[:, 0:TC], lhsT=ones[:], rhs=brow[:], start=True, stop=True)
-                nc.vector.tensor_copy(out=bias[:], in_=bank[:, 0:TC])
-            if 0 <= k - 1 < STEPS:
-                xq[k - 1] = quantise(xg[k - 1], 2048, p3, "x")
-            if 0 <= k - 2 < STEPS:
-                add_bias(k - 2)
-            if 0 <= k - 1 < STEPS:
+                nc.scalar.copy(out=bias[:], in_=bank[:, 0:TC])
+            if k == 1:
+                quantise_x(0)
+                first_product(0)
+            if live(k - 1):
+                transpose_beta(k - 1)
+            if k == 2:
+                add_bias(0)
+                quantise_x(1)
+            elif k > 2:
+                if live(k - 1):
+                    quantise_x(k - 1)
+                if live(k - 2):
+                    add_bias(k - 2)
+            if k >= 2 and live(k - 1):
                 first_product(k - 1)
-                bq[k - 1] = quantise(bg[k - 1], 1024, p6, "b")
-            if 0 <= k - 2 < STEPS:
+            if live(k - 2):
+                bq[k - 2] = quantise(bg[k - 2], 1024, p6, "b")
                 vq[k - 2] = quantise(vg[k - 2], 1024, p6, "v")
-            if k >= 4 and k % 2 == 0:
+            if k >= 4 and k % 2 == 0 and k < STEPS + 2:
                 second_product((k - 4) // 2)
+            if k == STEPS + 1:
+                last_product(0)
+            if k == STEPS + 2:
+                last_product(1)

@@ -172,7 +172,7 @@ def tile_text2imgca_pb_t_kernel(tc, beta, x2, Wv, bv, out):
             for h in range(2):
                 for g in range(2):
                     second_pass(bank[:, 256 * h:256 * h + 256], b, g, h)
-            o_t = p6.tile([P, 512], F32, name="o_sb")
+            o_t = res.tile([P, 512], F32, name="o_sb%d" % b)
             nc.scalar.copy(out=o_t[:], in_=bank[:])
             nc.sync.dma_start(out=out[b].rearrange("(p h) n -> p (h n)", h=2), in_=o_t[:])
 

@@ -14,7 +14,7 @@ P = 128
 B, NW, M, IC, TC = 12, 256, 1024, 512, 256
 STEPS = 2 * B
 FLOPS = 2 * B * M * IC * TC + 2 * B * NW * M * TC
-MANUAL = True
+MANUAL = False
 
 
 def tile_text2imgca_pb_t_kernel(tc, beta, x2, Wv, bv, out):

@@ -8,225 +8,232 @@ BF16 = mybir.dt.bfloat16
 U32 = mybir.dt.uint32
 U8 = mybir.dt.uint8
 FP8X4 = mybir.dt.float8_e4m3fn_x4
-ADD = mybir.AluOpType.add
 
 P = 128
-B, NW, M, IC, TC = 12, 256, 1024, 512, 256
-STEPS = 2 * B
-FLOPS = 2 * B * M * IC * TC + 2 * B * NW * M * TC
-MANUAL = False
+PACK = 4
+BATCH, WORDS, PIXELS, CHANNELS, TEXT = 12, 256, 1024, 512, 256
+K_PASS = P * PACK
+BANK = 512
+STEPS_PER_ENTRY = PIXELS // K_PASS
+STEPS = BATCH * STEPS_PER_ENTRY
+X_COLS = K_PASS * PACK
+BETA_COLS = WORDS * PACK
+V_COLS = TEXT * PACK
+BETA_AT = X_COLS
+V_AT = X_COLS + BETA_COLS
+STAGE_COLS = X_COLS + BETA_COLS + V_COLS
+X_LAG = 1
+V_LAG = 4
+BETA_TRANSPOSE_LAG = 2
+BIAS_LAG = 2
+
+FLOPS = 2 * BATCH * PIXELS * CHANNELS * TEXT + 2 * BATCH * WORDS * PIXELS * TEXT
 
 
 def tile_text2imgca_pb_t_kernel(tc, beta, x2, Wv, bv, out):
     nc = tc.nc
     with ExitStack() as ctx:
-        res = ctx.enter_context(tc.tile_pool(name="res", bufs=1))
-        p3 = ctx.enter_context(tc.tile_pool(name="p3", bufs=3))
-        p6 = ctx.enter_context(tc.tile_pool(name="p6", bufs=6))
-        ps_tr = ctx.enter_context(tc.psum_pool(name="ps_tr", bufs=4))
-        ps_v = ctx.enter_context(tc.psum_pool(name="ps_v", bufs=3))
-        ps_o = ctx.enter_context(tc.psum_pool(name="ps_o", bufs=1))
-        if MANUAL:
-            ctx.enter_context(tc.manual_schedule())
+        keep = ctx.enter_context(tc.tile_pool(name="keep", bufs=1))
+        rounds = ctx.enter_context(tc.tile_pool(name="rounds", bufs=4))
+        transposed = ctx.enter_context(tc.psum_pool(name="transposed", bufs=4))
+        v_sums = ctx.enter_context(tc.psum_pool(name="v_sums", bufs=3))
+        out_sums = ctx.enter_context(tc.psum_pool(name="out_sums", bufs=1))
+        ctx.enter_context(tc.manual_schedule())
 
-        x_sb = []
-        b_sb = []
+        x_in = []
         for s in range(STEPS):
-            x_t = res.tile([P, 2048], BF16, name="x%d" % s)
-            x_sb.append(x_t)
-        for b in range(B):
-            b_t = res.tile([P, 2048], BF16, name="b%d" % b)
-            b_sb.append(b_t)
-        w_raw = res.tile([P, 1024], BF16, name="w_raw")
-        w_grp = res.tile([P, 1024], BF16, name="w_grp", align_bytes=64)
-        w_codes = res.tile([P, 256], U32, name="w_codes", align_bytes=64)
-        w_scales = res.tile([P, 256], U8, name="w_scales", align_bytes=64)
-        brow = res.tile([P, TC], BF16, name="brow")
-        ones = res.tile([P, P], BF16, name="ones")
-        bias = res.tile([P, TC], F32, name="bias")
-        ident = res.tile([P, P], F32, name="ident")
+            x_t = keep.tile([P, K_PASS * CHANNELS // P], BF16, name="x%d" % s)
+            x_in.append(x_t)
+        beta_in = []
+        for b in range(BATCH):
+            beta_t = keep.tile([P, WORDS * PIXELS // P], BF16, name="beta%d" % b)
+            beta_in.append(beta_t)
+        w_rows = keep.tile([P, PACK * TEXT], BF16, name="w_rows")
+        w_stage = keep.tile([P, TEXT * PACK], BF16, name="w_stage", align_bytes=64)
+        w_codes = keep.tile([P, TEXT], U32, name="w_codes", align_bytes=64)
+        w_scales = keep.tile([P, TEXT], U8, name="w_scales", align_bytes=64)
+        bias_row = keep.tile([P, TEXT], BF16, name="bias_row")
+        ones = keep.tile([P, P], BF16, name="ones")
+        bias = keep.tile([P, TEXT], F32, name="bias")
+        identity = keep.tile([P, P], F32, name="identity")
 
-        nc.vector.memset(brow[:], 0.0)
+        nc.vector.memset(bias_row[:], 0.0)
         nc.vector.memset(ones[:], 1.0)
-        masks.make_identity(nc, ident[:])
+        masks.make_identity(nc, identity[:])
+
 
         def load_x(s):
-            b, g = divmod(s, 2)
-            src = x2[b].rearrange("h w c -> (h w) c").rearrange("(a p e) c -> p a (e c)", a=4, p=P, e=2)
+            b, g = divmod(s, STEPS_PER_ENTRY)
+            pixels = x2[b].rearrange("h w c -> (h w) c").rearrange("(a p e) c -> p a (e c)", a=4, p=P, e=2)
             nc.sync.dma_start(
-                out=x_sb[s][:].rearrange("p (a f) -> p a f", a=2), in_=src[:, 2 * g:2 * g + 2, :]
+                out=x_in[s][:].rearrange("p (a f) -> p a f", a=2), in_=pixels[:, 2 * g:2 * g + 2, :]
             )
 
         def load_beta(b):
-            nc.sync.dma_start(out=b_sb[b][:], in_=beta[b].rearrange("(p h) m -> p (h m)", h=2))
+            nc.sync.dma_start(out=beta_in[b][:], in_=beta[b].rearrange("(p h) m -> p (h m)", h=2))
 
         load_x(0)
         nc.sync.dma_start(
-            out=w_raw[:].rearrange("q (u f) -> q u f", u=2),
+            out=w_rows[:].rearrange("q (u f) -> q u f", u=2),
             in_=Wv.rearrange("(u q e) n -> q u (e n)", u=2, q=P, e=2),
         )
-        nc.sync.dma_start(out=brow[0:1, :], in_=bv.rearrange("(o n) -> o n", o=1))
-        load_x(1)
-        load_beta(0)
-        for b in range(1, B):
-            load_x(2 * b)
-            load_x(2 * b + 1)
-            load_beta(b)
+        nc.sync.dma_start(out=bias_row[0:1, :], in_=bv.rearrange("(o n) -> o n", o=1))
+        for s in range(1, STEPS):
+            load_x(s)
+            if s >= BETA_TRANSPOSE_LAG and s % STEPS_PER_ENTRY == 0:
+                load_beta((s - BETA_TRANSPOSE_LAG) // STEPS_PER_ENTRY)
+        load_beta(BATCH - 1)
 
         nc.vector.tensor_copy(
-            out=w_grp[:].rearrange("q (n t) -> q n t", t=4),
-            in_=w_raw[:].rearrange("q (t n) -> q n t", t=4),
+            out=w_stage[:].rearrange("q (n j) -> q n j", j=PACK),
+            in_=w_rows[:].rearrange("q (j n) -> q n j", j=PACK),
         )
-        nc.vector.quantize_mx(out=w_codes[:].bitcast(FP8X4), scales=w_scales[:], in_=w_grp[:])
+        nc.vector.quantize_mx(out=w_codes[:].bitcast(FP8X4), scales=w_scales[:], in_=w_stage[:])
 
-        xg = {}
-        bg = {}
-        xq = {}
-        bq = {}
-        vbank = {}
-        vg = {}
-        vq = {}
-
-        def out_of_bank(dst_bf16, bank):
-            nc.scalar.copy(
-                out=dst_bf16.bitcast(F32).rearrange("q (i m u) -> q i m u", i=2, u=2),
-                in_=bank[:].rearrange("q (i u m) -> q i m u", i=2, u=2),
-            )
-
-        def transpose_x(s):
-            xw = x_sb[s][:].bitcast(F32)
-            xg_t = p3.tile([P, 2048], BF16, name="xg", align_bytes=64)
-            xg[s] = xg_t
-            for half in range(2):
-                bank = ps_tr.tile([P, 512], F32, name="tr")
-                for i in range(4):
-                    c0 = 512 * half + 128 * i
-                    nc.tensor.transpose(bank[:, 128 * i:128 * i + 128], xw[:, c0:c0 + 128], ident[:])
-                out_of_bank(xg_t[:, 1024 * half:1024 * half + 1024], bank)
-
-        def transpose_beta(s):
-            b, g = divmod(s, 2)
-            bw = b_sb[b][:].bitcast(F32)
-            bg_t = p3.tile([P, 1024], BF16, name="bg", align_bytes=64)
-            bg[s] = bg_t
-            bank = ps_tr.tile([P, 512], F32, name="tr")
-            for h in range(2):
-                for u in range(2):
-                    c0 = 512 * h + 128 * (2 * g + u)
-                    d0 = (2 * h + u) * 128
-                    nc.tensor.transpose(bank[:, d0:d0 + 128], bw[:, c0:c0 + 128], ident[:])
-            out_of_bank(bg_t[:], bank)
-
-        def quantise(src, width, pool, label):
-            codes = pool.tile([P, width // 4], U32, name=label + "c", align_bytes=64)
-            scales = pool.tile([P, width // 4], U8, name=label + "s", align_bytes=64)
-            nc.vector.quantize_mx(out=codes[:].bitcast(FP8X4), scales=scales[:], in_=src[:])
-            return codes, scales
-
-        def quantise_x(s):
-            xq[s] = quantise(xg[s], 2048, p3, "x")
-
-        def first_product(s):
-            codes, scales = xq[s]
-            banks = []
-            for hf in range(2):
-                bank = ps_v.tile([P, 512], F32, name="v")
-                for t in range(4):
-                    nc.tensor.matmul_mx(
-                        out=bank[:, 128 * t:128 * t + 128],
-                        lhsT=codes[:, 128 * t:128 * t + 128].bitcast(FP8X4),
-                        lhsT_scale=scales[:, 128 * t:128 * t + 128],
-                        rhs=w_codes[:, 128 * hf:128 * hf + 128].bitcast(FP8X4),
-                        rhs_scale=w_scales[:, 128 * hf:128 * hf + 128],
-                        start=True,
-                        stop=True,
-                    )
-                banks.append(bank)
-            vbank[s] = banks
-
-        def add_bias(s):
-            vg_t = p3.tile([P, 1024], BF16, name="vg", align_bytes=64)
-            vg[s] = vg_t
-            for hf in range(2):
-                nc.vector.tensor_tensor(
-                    out=vg_t[:, 512 * hf:512 * hf + 512].rearrange("p (w t) -> p w t", t=4),
-                    in0=vbank[s][hf][:].rearrange("p (t w) -> p w t", t=4),
-                    in1=bias[:, 128 * hf:128 * hf + 128].unsqueeze(2).to_broadcast([P, 128, 4]),
-                    op=ADD,
-                )
-
-        def second_pass(acc, b, g, h):
-            s = 2 * b + g
-            nc.tensor.matmul_mx(
-                out=acc,
-                lhsT=bq[s][0][:, 128 * h:128 * h + 128].bitcast(FP8X4),
-                lhsT_scale=bq[s][1][:, 128 * h:128 * h + 128],
-                rhs=vq[s][0][:].bitcast(FP8X4),
-                rhs_scale=vq[s][1][:],
-                start=(g == 0),
-                stop=(g == 1),
-            )
-
-        def second_product(b):
-            bank = ps_o.tile([P, 512], F32, name="o")
-            for h in range(2):
-                for g in range(2):
-                    second_pass(bank[:, 256 * h:256 * h + 256], b, g, h)
-            o_t = res.tile([P, 512], F32, name="o_sb%d" % b)
-            nc.scalar.copy(out=o_t[:], in_=bank[:])
-            nc.sync.dma_start(out=out[b].rearrange("(p h) n -> p (h n)", h=2), in_=o_t[:])
-
-        last = []
-
-        def last_product(g):
-            b = B - 1
-            if g == 0:
-                bank0 = ps_o.tile([P, 512], F32, name="o")
-                bank1 = ps_tr.tile([P, 512], F32, name="tr")
-                last.append(bank0)
-                last.append(bank1)
-            for h in range(2):
-                second_pass(last[h][:, 0:256], b, g, h)
-            if g == 1:
-                dst = out[b].rearrange("(p h) n -> p h n", h=2)
-                o0 = res.tile([P, 256], F32, name="o_last0")
-                o1 = res.tile([P, 256], F32, name="o_last1")
-                nc.scalar.copy(out=o0[:], in_=last[0][:, 0:256])
-                nc.sync.dma_start(out=dst[:, 0, :], in_=o0[:])
-                nc.vector.tensor_copy(out=o1[:], in_=last[1][:, 0:256])
-                nc.sync.dma_start(out=dst[:, 1, :], in_=o1[:])
+        stage = {}
+        quantised = {}
+        v_banks = {}
 
         def live(s):
             return 0 <= s < STEPS
 
-        for k in range(STEPS + 3):
-            if live(k):
-                transpose_x(k)
-            if k == 0:
-                bank = ps_o.tile([P, 512], F32, name="o")
-                nc.tensor.matmul(out=bank[:, 0:TC], lhsT=ones[:], rhs=brow[:], start=True, stop=True)
-                nc.scalar.copy(out=bias[:], in_=bank[:, 0:TC])
-            if k == 1:
-                quantise_x(0)
-                first_product(0)
-            if live(k - 1):
-                transpose_beta(k - 1)
-            if k == 2:
-                add_bias(0)
-                quantise_x(1)
-            elif k > 2:
-                if live(k - 1):
-                    quantise_x(k - 1)
-                if live(k - 2):
-                    add_bias(k - 2)
-            if k >= 2 and live(k - 1):
-                first_product(k - 1)
-            if live(k - 2):
-                bq[k - 2] = quantise(bg[k - 2], 1024, p6, "b")
-                vq[k - 2] = quantise(vg[k - 2], 1024, p6, "v")
-            if k >= 4 and k % 2 == 0 and k < STEPS + 2:
-                second_product((k - 4) // 2)
-            if k == STEPS + 1:
-                last_product(0)
-            if k == STEPS + 2:
-                last_product(1)
+        def stage_tile(r):
+            if r not in stage:
+                stage_t = rounds.tile([P, STAGE_COLS], BF16, name="stage", align_bytes=64)
+                stage[r] = stage_t
+            return stage[r]
+
+        def words_out_of_bank(dst, bank):
+            nc.scalar.copy(
+                out=dst.bitcast(F32).rearrange("q (i m u) -> q i m u", i=2, u=2),
+                in_=bank[:].rearrange("q (i u m) -> q i m u", i=2, u=2),
+            )
+
+        def transpose_x(s):
+            words = x_in[s][:].bitcast(F32)
+            dst = stage_tile(s + X_LAG)
+            for half in range(2):
+                bank = transposed.tile([P, BANK], F32, name="tr")
+                for i in range(4):
+                    at = BANK * half + P * i
+                    nc.tensor.transpose(bank[:, P * i:P * i + P], words[:, at:at + P], identity[:])
+                words_out_of_bank(dst[:, X_COLS // 2 * half:X_COLS // 2 * (half + 1)], bank)
+
+        def transpose_beta(s):
+            b, g = divmod(s, STEPS_PER_ENTRY)
+            words = beta_in[b][:].bitcast(F32)
+            dst = stage_tile(s + V_LAG)
+            bank = transposed.tile([P, BANK], F32, name="tr")
+            for h in range(2):
+                for u in range(2):
+                    at = PIXELS // 2 * h + P * (2 * g + u)
+                    to = P * (2 * h + u)
+                    nc.tensor.transpose(bank[:, to:to + P], words[:, at:at + P], identity[:])
+            words_out_of_bank(dst[:, BETA_AT:BETA_AT + BETA_COLS], bank)
+
+        def quantise_round(r):
+            lo = 0 if live(r - X_LAG) else BETA_AT
+            hi = STAGE_COLS if live(r - V_LAG) else BETA_AT
+            codes = rounds.tile([P, STAGE_COLS // PACK], U32, name="codes", align_bytes=64)
+            scales = rounds.tile([P, STAGE_COLS // PACK], U8, name="scales", align_bytes=64)
+            nc.vector.quantize_mx(
+                out=codes[:, lo // PACK:hi // PACK].bitcast(FP8X4),
+                scales=scales[:, lo // PACK:hi // PACK],
+                in_=stage[r][:, lo:hi],
+            )
+            quantised[r] = (codes, scales)
+
+        def first_product(s):
+            codes, scales = quantised[s + X_LAG]
+            banks = []
+            for half in range(2):
+                bank = v_sums.tile([P, BANK], F32, name="v")
+                for j in range(PACK):
+                    nc.tensor.matmul_mx(
+                        out=bank[:, P * j:P * j + P],
+                        lhsT=codes[:, P * j:P * j + P].bitcast(FP8X4),
+                        lhsT_scale=scales[:, P * j:P * j + P],
+                        rhs=w_codes[:, P * half:P * half + P].bitcast(FP8X4),
+                        rhs_scale=w_scales[:, P * half:P * half + P],
+                        start=True,
+                        stop=True,
+                    )
+                banks.append(bank)
+            v_banks[s] = banks
+
+        def add_bias(s):
+            dst = stage_tile(s + V_LAG)
+            for half in range(2):
+                at = V_AT + V_COLS // 2 * half
+                nc.vector.tensor_tensor(
+                    out=dst[:, at:at + V_COLS // 2].rearrange("p (n j) -> p n j", j=PACK),
+                    in0=v_banks[s][half][:].rearrange("p (j n) -> p n j", j=PACK),
+                    in1=bias[:, P * half:P * half + P].unsqueeze(2).to_broadcast([P, P, PACK]),
+                    op=mybir.AluOpType.add,
+                )
+
+        def second_pass(sums, s, h):
+            codes, scales = quantised[s + V_LAG]
+            beta_at = BETA_AT // PACK + P * h
+            v_at = V_AT // PACK
+            nc.tensor.matmul_mx(
+                out=sums,
+                lhsT=codes[:, beta_at:beta_at + P].bitcast(FP8X4),
+                lhsT_scale=scales[:, beta_at:beta_at + P],
+                rhs=codes[:, v_at:v_at + TEXT].bitcast(FP8X4),
+                rhs_scale=scales[:, v_at:v_at + TEXT],
+                start=(s % STEPS_PER_ENTRY == 0),
+                stop=(s % STEPS_PER_ENTRY == STEPS_PER_ENTRY - 1),
+            )
+
+        def second_product(b):
+            bank = out_sums.tile([P, BANK], F32, name="o")
+            for h in range(2):
+                for g in range(STEPS_PER_ENTRY):
+                    second_pass(bank[:, TEXT * h:TEXT * h + TEXT], STEPS_PER_ENTRY * b + g, h)
+            result = keep.tile([P, 2 * TEXT], F32, name="out%d" % b)
+            nc.scalar.copy(out=result[:], in_=bank[:])
+            nc.sync.dma_start(out=out[b].rearrange("(p h) n -> p (h n)", h=2), in_=result[:])
+
+        last_banks = []
+
+        def last_product(g):
+            b = BATCH - 1
+            if g == 0:
+                bank0 = out_sums.tile([P, BANK], F32, name="o")
+                bank1 = transposed.tile([P, BANK], F32, name="tr")
+                last_banks.append(bank0)
+                last_banks.append(bank1)
+            for h in range(2):
+                second_pass(last_banks[h][:, 0:TEXT], STEPS_PER_ENTRY * b + g, h)
+            if g == STEPS_PER_ENTRY - 1:
+                rows = out[b].rearrange("(p h) n -> p h n", h=2)
+                result0 = keep.tile([P, TEXT], F32, name="out_last0")
+                result1 = keep.tile([P, TEXT], F32, name="out_last1")
+                nc.scalar.copy(out=result0[:], in_=last_banks[0][:, 0:TEXT])
+                nc.sync.dma_start(out=rows[:, 0, :], in_=result0[:])
+                nc.vector.tensor_copy(out=result1[:], in_=last_banks[1][:, 0:TEXT])
+                nc.sync.dma_start(out=rows[:, 1, :], in_=result1[:])
+
+        for r in range(STEPS + V_LAG):
+            if live(r):
+                transpose_x(r)
+            if r == 0:
+                bank = out_sums.tile([P, BANK], F32, name="o")
+                nc.tensor.matmul(out=bank[:, 0:TEXT], lhsT=ones[:], rhs=bias_row[:], start=True, stop=True)
+                nc.scalar.copy(out=bias[:], in_=bank[:, 0:TEXT])
+            if live(r - BETA_TRANSPOSE_LAG):
+                transpose_beta(r - BETA_TRANSPOSE_LAG)
+            if r >= X_LAG:
+                quantise_round(r)
+            if live(r - BIAS_LAG):
+                add_bias(r - BIAS_LAG)
+            if live(r - X_LAG):
+                first_product(r - X_LAG)
+            s_done = r - V_LAG
+            if live(s_done):
+                b, g = divmod(s_done, STEPS_PER_ENTRY)
+                if b == BATCH - 1:
+                    last_product(g)
+                elif g == STEPS_PER_ENTRY - 1:
+                    second_product(b)

@@ -26,6 +26,7 @@ X_LAG = 1
 V_LAG = 4
 BETA_TRANSPOSE_LAG = 2
 BIAS_LAG = 2
+AHEAD_FROM = 4
 
 FLOPS = 2 * BATCH * PIXELS * CHANNELS * TEXT + 2 * BATCH * WORDS * PIXELS * TEXT
 
@@ -96,6 +97,15 @@ def tile_text2imgca_pb_t_kernel(tc, beta, x2, Wv, bv, out):
 
         def live(s):
             return 0 <= s < STEPS
+
+        def x_steps_of_round(r):
+            if r < AHEAD_FROM:
+                steps = [r]
+            elif r == AHEAD_FROM:
+                steps = [r, r + 1]
+            else:
+                steps = [r + 1]
+            return [s for s in steps if live(s)]
 
         def stage_tile(r):
             if r not in stage:
@@ -216,8 +226,8 @@ def tile_text2imgca_pb_t_kernel(tc, beta, x2, Wv, bv, out):
                 nc.sync.dma_start(out=rows[:, 1, :], in_=result1[:])
 
         for r in range(STEPS + V_LAG):
-            if live(r):
-                transpose_x(r)
+            for s in x_steps_of_round(r):
+                transpose_x(s)
             if r == 0:
                 bank = out_sums.tile([P, BANK], F32, name="o")
                 nc.tensor.matmul(out=bank[:, 0:TEXT], lhsT=ones[:], rhs=bias_row[:], start=True, stop=True)

@@ -19,14 +19,8 @@ STEPS = BATCH * STEPS_PER_ENTRY
 X_COLS = K_PASS * PACK
 BETA_COLS = WORDS * PACK
 V_COLS = TEXT * PACK
-BETA_AT = X_COLS
-V_AT = X_COLS + BETA_COLS
-STAGE_COLS = X_COLS + BETA_COLS + V_COLS
-X_LAG = 1
-V_LAG = 4
-BETA_TRANSPOSE_LAG = 2
-BIAS_LAG = 2
-AHEAD_FROM = 4
+V_AT = STEPS_PER_ENTRY * BETA_COLS
+X_SLOTS = 20
 
 FLOPS = 2 * BATCH * PIXELS * CHANNELS * TEXT + 2 * BATCH * WORDS * PIXELS * TEXT
 
@@ -35,16 +29,17 @@ def tile_text2imgca_pb_t_kernel(tc, beta, x2, Wv, bv, out):
     nc = tc.nc
     with ExitStack() as ctx:
         keep = ctx.enter_context(tc.tile_pool(name="keep", bufs=1))
-        rounds = ctx.enter_context(tc.tile_pool(name="rounds", bufs=4))
+        rounds = ctx.enter_context(tc.tile_pool(name="rounds", bufs=2))
         transposed = ctx.enter_context(tc.psum_pool(name="transposed", bufs=4))
-        v_sums = ctx.enter_context(tc.psum_pool(name="v_sums", bufs=3))
-        out_sums = ctx.enter_context(tc.psum_pool(name="out_sums", bufs=1))
+        v_sums = ctx.enter_context(tc.psum_pool(name="v_sums", bufs=4))
         ctx.enter_context(tc.manual_schedule())
 
         x_in = []
-        for s in range(STEPS):
+        for s in range(X_SLOTS):
             x_t = keep.tile([P, K_PASS * CHANNELS // P], BF16, name="x%d" % s)
             x_in.append(x_t)
+        for s in range(X_SLOTS, STEPS):
+            x_in.append(x_in[s - X_SLOTS])
         beta_in = []
         for b in range(BATCH):
             beta_t = keep.tile([P, WORDS * PIXELS // P], BF16, name="beta%d" % b)
@@ -58,6 +53,8 @@ def tile_text2imgca_pb_t_kernel(tc, beta, x2, Wv, bv, out):
         bias = keep.tile([P, TEXT], F32, name="bias")
         identity = keep.tile([P, P], F32, name="identity")
 
+        warm = keep.tile([P, BANK], BF16, name="warm")
+        nc.vector.memset(warm[:], 0.0)
         nc.vector.memset(bias_row[:], 0.0)
         nc.vector.memset(ones[:], 1.0)
         masks.make_identity(nc, identity[:])
@@ -73,17 +70,19 @@ def tile_text2imgca_pb_t_kernel(tc, beta, x2, Wv, bv, out):
         def load_beta(b):
             nc.sync.dma_start(out=beta_in[b][:], in_=beta[b].rearrange("(p h) m -> p (h m)", h=2))
 
-        load_x(0)
         nc.sync.dma_start(
             out=w_rows[:].rearrange("q (u f) -> q u f", u=2),
             in_=Wv.rearrange("(u q e) n -> q u (e n)", u=2, q=P, e=2),
         )
+        load_x(0)
         nc.sync.dma_start(out=bias_row[0:1, :], in_=bv.rearrange("(o n) -> o n", o=1))
-        for s in range(1, STEPS):
+        def load_step(s):
             load_x(s)
-            if s >= BETA_TRANSPOSE_LAG and s % STEPS_PER_ENTRY == 0:
-                load_beta((s - BETA_TRANSPOSE_LAG) // STEPS_PER_ENTRY)
-        load_beta(BATCH - 1)
+            if s >= 5 and s % STEPS_PER_ENTRY == 1:
+                load_beta((s - 5) // STEPS_PER_ENTRY)
+
+        for s in range(1, X_SLOTS):
+            load_step(s)
 
         nc.vector.tensor_copy(
             out=w_stage[:].rearrange("q (n j) -> q n j", j=PACK),
@@ -91,116 +90,119 @@ def tile_text2imgca_pb_t_kernel(tc, beta, x2, Wv, bv, out):
         )
         nc.vector.quantize_mx(out=w_codes[:].bitcast(FP8X4), scales=w_scales[:], in_=w_stage[:])
 
-        stage = {}
-        quantised = {}
+        x_stage = {}
+        x_coded = {}
+        bv_stage = {}
+        bv_coded = {}
         v_banks = {}
 
-        def live(s):
-            return 0 <= s < STEPS
+        def stage_of(table, b, name):
+            if b not in table:
+                stage_t = rounds.tile([P, STEPS_PER_ENTRY * X_COLS], BF16, name=name, align_bytes=64, bufs=2 if name == "x_stage" else 3)
+                table[b] = stage_t
+            return table[b]
 
-        def x_steps_of_round(r):
-            if r < AHEAD_FROM:
-                steps = [r]
-            elif r == AHEAD_FROM:
-                steps = [r, r + 1]
+        def codes_of(table, b, name):
+            if b not in table:
+                codes = rounds.tile([P, K_PASS * STEPS_PER_ENTRY], U32, name=name + "_codes", align_bytes=64)
+                scales = rounds.tile([P, K_PASS * STEPS_PER_ENTRY], U8, name=name + "_scales", align_bytes=64)
+                table[b] = (codes, scales)
+            return table[b]
+
+        def words_out_of_bank(dst, bank, on_vector=False):
+            o = dst.bitcast(F32).rearrange("q (i m u) -> q i m u", i=2, u=2)
+            i = bank[:].rearrange("q (i u m) -> q i m u", i=2, u=2)
+            if on_vector:
+                nc.vector.tensor_copy(out=o, in_=i)
             else:
-                steps = [r + 1]
-            return [s for s in steps if live(s)]
+                nc.scalar.copy(out=o, in_=i)
 
-        def stage_tile(r):
-            if r not in stage:
-                stage_t = rounds.tile([P, STAGE_COLS], BF16, name="stage", align_bytes=64)
-                stage[r] = stage_t
-            return stage[r]
-
-        def words_out_of_bank(dst, bank):
-            nc.scalar.copy(
-                out=dst.bitcast(F32).rearrange("q (i m u) -> q i m u", i=2, u=2),
-                in_=bank[:].rearrange("q (i u m) -> q i m u", i=2, u=2),
-            )
-
-        def transpose_x(s):
+        def transpose_x(s, on_vector=(False, False)):
+            b, g = divmod(s, STEPS_PER_ENTRY)
             words = x_in[s][:].bitcast(F32)
-            dst = stage_tile(s + X_LAG)
+            dst = stage_of(x_stage, b, "x_stage")
             for half in range(2):
                 bank = transposed.tile([P, BANK], F32, name="tr")
                 for i in range(4):
                     at = BANK * half + P * i
                     nc.tensor.transpose(bank[:, P * i:P * i + P], words[:, at:at + P], identity[:])
-                words_out_of_bank(dst[:, X_COLS // 2 * half:X_COLS // 2 * (half + 1)], bank)
+                to = X_COLS * g + X_COLS // 2 * half
+                words_out_of_bank(dst[:, to:to + X_COLS // 2], bank, on_vector[half])
 
-        def transpose_beta(s):
-            b, g = divmod(s, STEPS_PER_ENTRY)
+        def transpose_beta(b):
             words = beta_in[b][:].bitcast(F32)
-            dst = stage_tile(s + V_LAG)
-            bank = transposed.tile([P, BANK], F32, name="tr")
-            for h in range(2):
-                for u in range(2):
-                    at = PIXELS // 2 * h + P * (2 * g + u)
-                    to = P * (2 * h + u)
-                    nc.tensor.transpose(bank[:, to:to + P], words[:, at:at + P], identity[:])
-            words_out_of_bank(dst[:, BETA_AT:BETA_AT + BETA_COLS], bank)
+            dst = stage_of(bv_stage, b, "bv_stage")
+            for g in range(STEPS_PER_ENTRY):
+                bank = transposed.tile([P, BANK], F32, name="tr")
+                for h in range(2):
+                    for u in range(2):
+                        at = PIXELS // 2 * h + P * (2 * g + u)
+                        to = P * (2 * h + u)
+                        nc.tensor.transpose(bank[:, to:to + P], words[:, at:at + P], identity[:])
+                words_out_of_bank(dst[:, BETA_COLS * g:BETA_COLS * (g + 1)], bank)
 
-        def quantise_round(r):
-            lo = 0 if live(r - X_LAG) else BETA_AT
-            hi = STAGE_COLS if live(r - V_LAG) else BETA_AT
-            codes = rounds.tile([P, STAGE_COLS // PACK], U32, name="codes", align_bytes=64)
-            scales = rounds.tile([P, STAGE_COLS // PACK], U8, name="scales", align_bytes=64)
+        def quantise(table, coded, b, name, lo, hi):
+            codes, scales = codes_of(coded, b, name)
             nc.vector.quantize_mx(
                 out=codes[:, lo // PACK:hi // PACK].bitcast(FP8X4),
                 scales=scales[:, lo // PACK:hi // PACK],
-                in_=stage[r][:, lo:hi],
+                in_=table[b][:, lo:hi],
             )
-            quantised[r] = (codes, scales)
 
-        def first_product(s):
-            codes, scales = quantised[s + X_LAG]
-            banks = []
-            for half in range(2):
-                bank = v_sums.tile([P, BANK], F32, name="v")
-                for j in range(PACK):
-                    nc.tensor.matmul_mx(
-                        out=bank[:, P * j:P * j + P],
-                        lhsT=codes[:, P * j:P * j + P].bitcast(FP8X4),
-                        lhsT_scale=scales[:, P * j:P * j + P],
-                        rhs=w_codes[:, P * half:P * half + P].bitcast(FP8X4),
-                        rhs_scale=w_scales[:, P * half:P * half + P],
-                        start=True,
-                        stop=True,
-                    )
-                banks.append(bank)
-            v_banks[s] = banks
+        def quantise_x(s, steps=1):
+            b, g = divmod(s, STEPS_PER_ENTRY)
+            quantise(x_stage, x_coded, b, "x", X_COLS * g, X_COLS * (g + steps))
 
-        def add_bias(s):
-            dst = stage_tile(s + V_LAG)
-            for half in range(2):
-                at = V_AT + V_COLS // 2 * half
-                nc.vector.tensor_tensor(
-                    out=dst[:, at:at + V_COLS // 2].rearrange("p (n j) -> p n j", j=PACK),
-                    in0=v_banks[s][half][:].rearrange("p (j n) -> p n j", j=PACK),
-                    in1=bias[:, P * half:P * half + P].unsqueeze(2).to_broadcast([P, P, PACK]),
-                    op=mybir.AluOpType.add,
+        def quantise_bv(b, lo=0, hi=STEPS_PER_ENTRY * X_COLS):
+            quantise(bv_stage, bv_coded, b, "bv", lo, hi)
+
+        def first_product(s, half):
+            b, g = divmod(s, STEPS_PER_ENTRY)
+            codes, scales = x_coded[b]
+            bank = v_sums.tile([P, BANK], F32, name="v")
+            for j in range(PACK):
+                at = K_PASS * g + P * j
+                nc.tensor.matmul_mx(
+                    out=bank[:, P * j:P * j + P],
+                    lhsT=codes[:, at:at + P].bitcast(FP8X4),
+                    lhsT_scale=scales[:, at:at + P],
+                    rhs=w_codes[:, P * half:P * half + P].bitcast(FP8X4),
+                    rhs_scale=w_scales[:, P * half:P * half + P],
+                    start=True,
+                    stop=True,
                 )
+            v_banks[s, half] = bank
 
-        def second_pass(sums, s, h):
-            codes, scales = quantised[s + V_LAG]
-            beta_at = BETA_AT // PACK + P * h
-            v_at = V_AT // PACK
+        def add_bias(s, half):
+            b, g = divmod(s, STEPS_PER_ENTRY)
+            dst = stage_of(bv_stage, b, "bv_stage")
+            at = V_AT + V_COLS * g + V_COLS // 2 * half
+            nc.vector.tensor_tensor(
+                out=dst[:, at:at + V_COLS // 2].rearrange("p (n j) -> p n j", j=PACK),
+                in0=v_banks[s, half][:].rearrange("p (j n) -> p n j", j=PACK),
+                in1=bias[:, P * half:P * half + P].unsqueeze(2).to_broadcast([P, P, PACK]),
+                op=mybir.AluOpType.add,
+            )
+
+        def second_pass(sums, b, g, h):
+            codes, scales = bv_coded[b]
+            beta_at = (BETA_COLS * g) // PACK + P * h
+            v_at = (V_AT + V_COLS * g) // PACK
             nc.tensor.matmul_mx(
                 out=sums,
                 lhsT=codes[:, beta_at:beta_at + P].bitcast(FP8X4),
                 lhsT_scale=scales[:, beta_at:beta_at + P],
                 rhs=codes[:, v_at:v_at + TEXT].bitcast(FP8X4),
                 rhs_scale=scales[:, v_at:v_at + TEXT],
-                start=(s % STEPS_PER_ENTRY == 0),
-                stop=(s % STEPS_PER_ENTRY == STEPS_PER_ENTRY - 1),
+                start=(g == 0),
+                stop=(g == STEPS_PER_ENTRY - 1),
             )
 
         def second_product(b):
-            bank = out_sums.tile([P, BANK], F32, name="o")
+            bank = transposed.tile([P, BANK], F32, name="tr")
             for h in range(2):
                 for g in range(STEPS_PER_ENTRY):
-                    second_pass(bank[:, TEXT * h:TEXT * h + TEXT], STEPS_PER_ENTRY * b + g, h)
+                    second_pass(bank[:, TEXT * h:TEXT * h + TEXT], b, g, h)
             result = keep.tile([P, 2 * TEXT], F32, name="out%d" % b)
             nc.scalar.copy(out=result[:], in_=bank[:])
             nc.sync.dma_start(out=out[b].rearrange("(p h) n -> p (h n)", h=2), in_=result[:])
@@ -210,12 +212,12 @@ def tile_text2imgca_pb_t_kernel(tc, beta, x2, Wv, bv, out):
         def last_product(g):
             b = BATCH - 1
             if g == 0:
-                bank0 = out_sums.tile([P, BANK], F32, name="o")
+                bank0 = transposed.tile([P, BANK], F32, name="tr")
                 bank1 = transposed.tile([P, BANK], F32, name="tr")
                 last_banks.append(bank0)
                 last_banks.append(bank1)
             for h in range(2):
-                second_pass(last_banks[h][:, 0:TEXT], STEPS_PER_ENTRY * b + g, h)
+                second_pass(last_banks[h][:, 0:TEXT], b, g, h)
             if g == STEPS_PER_ENTRY - 1:
                 rows = out[b].rearrange("(p h) n -> p h n", h=2)
                 result0 = keep.tile([P, TEXT], F32, name="out_last0")
@@ -225,25 +227,71 @@ def tile_text2imgca_pb_t_kernel(tc, beta, x2, Wv, bv, out):
                 nc.vector.tensor_copy(out=result1[:], in_=last_banks[1][:, 0:TEXT])
                 nc.sync.dma_start(out=rows[:, 1, :], in_=result1[:])
 
-        for r in range(STEPS + V_LAG):
-            for s in x_steps_of_round(r):
-                transpose_x(s)
-            if r == 0:
-                bank = out_sums.tile([P, BANK], F32, name="o")
-                nc.tensor.matmul(out=bank[:, 0:TEXT], lhsT=ones[:], rhs=bias_row[:], start=True, stop=True)
-                nc.scalar.copy(out=bias[:], in_=bank[:, 0:TEXT])
-            if live(r - BETA_TRANSPOSE_LAG):
-                transpose_beta(r - BETA_TRANSPOSE_LAG)
-            if r >= X_LAG:
-                quantise_round(r)
-            if live(r - BIAS_LAG):
-                add_bias(r - BIAS_LAG)
-            if live(r - X_LAG):
-                first_product(r - X_LAG)
-            s_done = r - V_LAG
-            if live(s_done):
-                b, g = divmod(s_done, STEPS_PER_ENTRY)
-                if b == BATCH - 1:
-                    last_product(g)
-                elif g == STEPS_PER_ENTRY - 1:
-                    second_product(b)
+        bank = transposed.tile([P, BANK], F32, name="tr")
+        for i in range(7):
+            nc.tensor.matmul(out=bank[:], lhsT=warm[:, 0:P], rhs=warm[:], start=True, stop=True)
+        def fp(s):
+            first_product(s, 0)
+            first_product(s, 1)
+
+        def ab(s):
+            add_bias(s, 0)
+            add_bias(s, 1)
+
+        transpose_x(0, (False, True))
+        bank = transposed.tile([P, BANK], F32, name="tr")
+        nc.tensor.matmul(out=bank[:, 0:TEXT], lhsT=ones[:], rhs=bias_row[:], start=True, stop=True)
+        nc.scalar.copy(out=bias[:], in_=bank[:, 0:TEXT])
+        quantise_x(0)
+        transpose_x(1, (False, False))
+        transpose_x(2, (False, False))
+        fp(0)
+        quantise_x(1)
+        transpose_x(3, (False, False))
+        ab(0)
+        fp(1)
+        quantise_x(2)
+        transpose_x(4)
+        ab(1)
+        fp(2)
+        transpose_x(5)
+        quantise_x(3)
+        ab(2)
+        fp(3)
+        ab(3)
+        for s in range(X_SLOTS, STEPS):
+            load_step(s)
+        load_beta(BATCH - 2)
+        load_beta(BATCH - 1)
+        transpose_beta(0)
+        quantise_x(4, 2)
+        transpose_x(6)
+        transpose_x(7)
+        for b in range(2, BATCH):
+            s = STEPS_PER_ENTRY * b
+            if b > 2:
+                quantise_x(s, 2)
+            quantise_bv(b - 2)
+            fp(s)
+            fp(s + 1)
+            second_product(b - 2)
+            ab(s)
+            if b < BATCH - 1:
+                transpose_beta(b - 1)
+            if b + 2 < BATCH:
+                transpose_x(s + 4)
+                transpose_x(s + 5)
+            if b == BATCH - 2:
+                transpose_beta(b)
+                transpose_beta(b + 1)
+            if b < BATCH - 1:
+                ab(s + 1)
+        b = BATCH - 1
+        quantise_bv(b - 1)
+        second_product(b - 1)
+        ab(STEPS - 1)
+        quantise_bv(b, 0, V_AT)
+        quantise_bv(b, V_AT, V_AT + V_COLS)
+        last_product(0)
+        quantise_bv(b, V_AT + V_COLS, V_AT + 2 * V_COLS)
+        last_product(1)

@@ -63,17 +63,25 @@ def tile_text2imgca_pb_t_kernel(tc, beta, x2, Wv, bv, out):
         def load_x(s):
             b, g = divmod(s, STEPS_PER_ENTRY)
             pixels = x2[b].rearrange("h w c -> (h w) c").rearrange("(a p e) c -> p a (e c)", a=4, p=P, e=2)
-            nc.sync.dma_start(
-                out=x_in[s][:].rearrange("p (a f) -> p a f", a=2), in_=pixels[:, 2 * g:2 * g + 2, :]
-            )
+            if s == 0:
+                for a in range(2):
+                    nc.sync.dma_start(out=x_in[s][:, 1024 * a:1024 * a + 1024], in_=pixels[:, 2 * g + a, :])
+                    if a == 0:
+                        load_w()
+            else:
+                nc.sync.dma_start(
+                    out=x_in[s][:].rearrange("p (a f) -> p a f", a=2), in_=pixels[:, 2 * g:2 * g + 2, :]
+                )
 
         def load_beta(b):
             nc.sync.dma_start(out=beta_in[b][:], in_=beta[b].rearrange("(p h) m -> p (h m)", h=2))
 
-        nc.sync.dma_start(
-            out=w_rows[:].rearrange("q (u f) -> q u f", u=2),
-            in_=Wv.rearrange("(u q e) n -> q u (e n)", u=2, q=P, e=2),
-        )
+        def load_w():
+            nc.sync.dma_start(
+                out=w_rows[:].rearrange("q (u f) -> q u f", u=2),
+                in_=Wv.rearrange("(u q e) n -> q u (e n)", u=2, q=P, e=2),
+            )
+
         load_x(0)
         nc.sync.dma_start(out=bias_row[0:1, :], in_=bv.rearrange("(o n) -> o n", o=1))
         def load_step(s):
@@ -117,11 +125,11 @@ def tile_text2imgca_pb_t_kernel(tc, beta, x2, Wv, bv, out):
             else:
                 nc.scalar.copy(out=o, in_=i)
 
-        def transpose_x(s, on_vector=(False, False)):
+        def transpose_x(s, part=None, on_vector=(False, False)):
             b, g = divmod(s, STEPS_PER_ENTRY)
             words = x_in[s][:].bitcast(F32)
             dst = stage_of(x_stage, b, "x_stage")
-            for half in range(2):
+            for half in range(2) if part is None else [part]:
                 bank = transposed.tile([P, BANK], F32, name="tr")
                 for i in range(4):
                     at = BANK * half + P * i
@@ -129,10 +137,10 @@ def tile_text2imgca_pb_t_kernel(tc, beta, x2, Wv, bv, out):
                 to = X_COLS * g + X_COLS // 2 * half
                 words_out_of_bank(dst[:, to:to + X_COLS // 2], bank, on_vector[half])
 
-        def transpose_beta(b):
+        def transpose_beta(b, part=None):
             words = beta_in[b][:].bitcast(F32)
             dst = stage_of(bv_stage, b, "bv_stage")
-            for g in range(STEPS_PER_ENTRY):
+            for g in range(STEPS_PER_ENTRY) if part is None else [part]:
                 bank = transposed.tile([P, BANK], F32, name="tr")
                 for h in range(2):
                     for u in range(2):
@@ -238,54 +246,56 @@ def tile_text2imgca_pb_t_kernel(tc, beta, x2, Wv, bv, out):
             add_bias(s, 0)
             add_bias(s, 1)
 
-        transpose_x(0, (False, True))
+        transpose_x(0, None, (False, True))
         bank = transposed.tile([P, BANK], F32, name="tr")
         nc.tensor.matmul(out=bank[:, 0:TEXT], lhsT=ones[:], rhs=bias_row[:], start=True, stop=True)
         nc.scalar.copy(out=bias[:], in_=bank[:, 0:TEXT])
         quantise_x(0)
-        transpose_x(1, (False, False))
-        transpose_x(2, (False, False))
+        transpose_x(1, None, (False, True))
+        transpose_x(2)
         fp(0)
         quantise_x(1)
-        transpose_x(3, (False, False))
-        ab(0)
+        transpose_x(3)
         fp(1)
+        ab(0)
         quantise_x(2)
         transpose_x(4)
-        ab(1)
         fp(2)
-        transpose_x(5)
+        ab(1)
         quantise_x(3)
-        ab(2)
+        transpose_x(5)
         fp(3)
-        ab(3)
         for s in range(X_SLOTS, STEPS):
             load_step(s)
         load_beta(BATCH - 2)
         load_beta(BATCH - 1)
         transpose_beta(0)
-        quantise_x(4, 2)
         transpose_x(6)
         transpose_x(7)
-        for b in range(2, BATCH):
+        for b in range(1, BATCH):
             s = STEPS_PER_ENTRY * b
-            if b > 2:
-                quantise_x(s, 2)
-            quantise_bv(b - 2)
-            fp(s)
-            fp(s + 1)
-            second_product(b - 2)
+            if b >= 2:
+                quantise_bv(b - 2)
             ab(s)
-            if b < BATCH - 1:
-                transpose_beta(b - 1)
-            if b + 2 < BATCH:
-                transpose_x(s + 4)
-                transpose_x(s + 5)
-            if b == BATCH - 2:
-                transpose_beta(b)
-                transpose_beta(b + 1)
-            if b < BATCH - 1:
+            if b + 1 < BATCH:
+                quantise_x(s + 2, 2)
+                fp(s + 2)
+                if b + 3 <= BATCH:
+                    transpose_beta(b, 0)
+                    transpose_beta(b, 1)
+                if b + 3 < BATCH:
+                    transpose_x(s + 6, 0)
+                elif b + 1 < BATCH:
+                    transpose_beta(b + 1, 0)
+                    transpose_beta(b + 1, 1)
                 ab(s + 1)
+                fp(s + 3)
+            if b >= 2:
+                second_product(b - 2)
+            if b + 3 < BATCH:
+                transpose_x(s + 6, 1)
+                transpose_x(s + 7, 0)
+                transpose_x(s + 7, 1)
         b = BATCH - 1
         quantise_bv(b - 1)
         second_product(b - 1)

@@ -192,6 +192,32 @@ def tile_text2imgca_pb_t_kernel(tc, beta, x2, Wv, bv, out):
                 op=mybir.AluOpType.add,
             )
 
+        def copy_v_out(s, half):
+            sums = rounds.tile([P, BANK], F32, name="sums")
+            nc.scalar.copy(
+                out=sums[:].rearrange("p (n j) -> p n j", j=PACK),
+                in_=v_banks[s, half][:].rearrange("p (j n) -> p n j", j=PACK),
+            )
+            v_banks[s, half] = sums
+
+        def add_bias_on_gpsimd(s, half):
+            b, g = divmod(s, STEPS_PER_ENTRY)
+            dst = stage_of(bv_stage, b, "bv_stage")
+            at = V_AT + V_COLS * g + V_COLS // 2 * half
+            nc.gpsimd.tensor_tensor(
+                out=dst[:, at:at + V_COLS // 2].rearrange("p (n j) -> p n j", j=PACK),
+                in0=v_banks[s, half][:].rearrange("p (n j) -> p n j", j=PACK),
+                in1=bias[:, P * half:P * half + P].unsqueeze(2).to_broadcast([P, P, PACK]),
+                op=mybir.AluOpType.add,
+            )
+
+        def gate_gpsimd(b):
+            gate = rounds.tile([P, 64], U8, name="gate")
+            nc.gpsimd.tensor_copy(out=gate[:], in_=bv_coded[b][1][:, 0:64])
+
+        def on_gpsimd(b):
+            return 2 <= b < BATCH - 2
+
         def second_pass(sums, b, g, h):
             codes, scales = bv_coded[b]
             beta_at = (BETA_COLS * g) // PACK + P * h
@@ -276,6 +302,9 @@ def tile_text2imgca_pb_t_kernel(tc, beta, x2, Wv, bv, out):
             s = STEPS_PER_ENTRY * b
             if b >= 2:
                 quantise_bv(b - 2)
+            if b >= 2 and on_gpsimd(b - 1):
+                gate_gpsimd(b - 2)
+                add_bias_on_gpsimd(s - 1, 1)
             ab(s)
             if b + 1 < BATCH:
                 quantise_x(s + 2, 2)
@@ -288,8 +317,12 @@ def tile_text2imgca_pb_t_kernel(tc, beta, x2, Wv, bv, out):
                 elif b + 1 < BATCH:
                     transpose_beta(b + 1, 0)
                     transpose_beta(b + 1, 1)
-                ab(s + 1)
+                add_bias(s + 1, 0)
+                if not on_gpsimd(b):
+                    add_bias(s + 1, 1)
                 fp(s + 3)
+                if on_gpsimd(b + 1):
+                    copy_v_out(s + 3, 1)
             if b >= 2:
                 second_product(b - 2)
             if b + 3 < BATCH:

@@ -62,16 +62,8 @@ def tile_text2imgca_pb_t_kernel(tc, beta, x2, Wv, bv, out):
 
         def load_x(s):
             b, g = divmod(s, STEPS_PER_ENTRY)
-            pixels = x2[b].rearrange("h w c -> (h w) c").rearrange("(a p e) c -> p a (e c)", a=4, p=P, e=2)
-            if s == 0:
-                for a in range(2):
-                    nc.sync.dma_start(out=x_in[s][:, 1024 * a:1024 * a + 1024], in_=pixels[:, 2 * g + a, :])
-                    if a == 0:
-                        load_w()
-            else:
-                nc.sync.dma_start(
-                    out=x_in[s][:].rearrange("p (a f) -> p a f", a=2), in_=pixels[:, 2 * g:2 * g + 2, :]
-                )
+            pixels = x2[b].rearrange("h w c -> (h w) c").rearrange("(g q i) c -> g q (i c)", g=2, q=P, i=4)
+            nc.sync.dma_start(out=x_in[s][:], in_=pixels[g])
 
         def load_beta(b):
             nc.sync.dma_start(out=beta_in[b][:], in_=beta[b].rearrange("(p h) m -> p (h m)", h=2))
@@ -82,6 +74,7 @@ def tile_text2imgca_pb_t_kernel(tc, beta, x2, Wv, bv, out):
                 in_=Wv.rearrange("(u q e) n -> q u (e n)", u=2, q=P, e=2),
             )
 
+        load_w()
         load_x(0)
         nc.sync.dma_start(out=bias_row[0:1, :], in_=bv.rearrange("(o n) -> o n", o=1))
         def load_step(s):
@@ -117,6 +110,14 @@ def tile_text2imgca_pb_t_kernel(tc, beta, x2, Wv, bv, out):
                 table[b] = (codes, scales)
             return table[b]
 
+        def x_out_of_bank(dst, bank, on_vector=False):
+            o = dst.bitcast(F32).rearrange("k (q i u) -> k q i u", i=2, u=2)
+            i = bank[:].rearrange("k (i u q) -> k q i u", i=2, u=2)
+            if on_vector:
+                nc.vector.tensor_copy(out=o, in_=i)
+            else:
+                nc.scalar.copy(out=o, in_=i)
+
         def words_out_of_bank(dst, bank, on_vector=False):
             o = dst.bitcast(F32).rearrange("q (i m u) -> q i m u", i=2, u=2)
             i = bank[:].rearrange("q (i u m) -> q i m u", i=2, u=2)
@@ -131,11 +132,13 @@ def tile_text2imgca_pb_t_kernel(tc, beta, x2, Wv, bv, out):
             dst = stage_of(x_stage, b, "x_stage")
             for half in range(2) if part is None else [part]:
                 bank = transposed.tile([P, BANK], F32, name="tr")
-                for i in range(4):
-                    at = BANK * half + P * i
-                    nc.tensor.transpose(bank[:, P * i:P * i + P], words[:, at:at + P], identity[:])
+                for i in range(2):
+                    for u in range(2):
+                        at = 2 * P * (half + 2 * i) + P * u
+                        to = P * (2 * i + u)
+                        nc.tensor.transpose(bank[:, to:to + P], words[:, at:at + P], identity[:])
                 to = X_COLS * g + X_COLS // 2 * half
-                words_out_of_bank(dst[:, to:to + X_COLS // 2], bank, on_vector[half])
+                x_out_of_bank(dst[:, to:to + X_COLS // 2], bank, on_vector[half])
 
         def transpose_beta(b, part=None):
             words = beta_in[b][:].bitcast(F32)
@@ -168,8 +171,9 @@ def tile_text2imgca_pb_t_kernel(tc, beta, x2, Wv, bv, out):
             b, g = divmod(s, STEPS_PER_ENTRY)
             codes, scales = x_coded[b]
             bank = v_sums.tile([P, BANK], F32, name="v")
-            for j in range(PACK):
-                at = K_PASS * g + P * j
+            for t in range(PACK):
+                at = K_PASS * g + P * t
+                j = 2 * (t % 2) + t // 2
                 nc.tensor.matmul_mx(
                     out=bank[:, P * j:P * j + P],
                     lhsT=codes[:, at:at + P].bitcast(FP8X4),

@@ -21,6 +21,7 @@ BETA_COLS = WORDS * PACK
 V_COLS = TEXT * PACK
 V_AT = STEPS_PER_ENTRY * BETA_COLS
 X_SLOTS = 20
+GP_FROM = 64
 
 FLOPS = 2 * BATCH * PIXELS * CHANNELS * TEXT + 2 * BATCH * WORDS * PIXELS * TEXT
 
@@ -185,39 +186,41 @@ def tile_text2imgca_pb_t_kernel(tc, beta, x2, Wv, bv, out):
                 )
             v_banks[s, half] = bank
 
-        def add_bias(s, half):
+        def add_bias(s, half, lo=0, hi=P):
             b, g = divmod(s, STEPS_PER_ENTRY)
             dst = stage_of(bv_stage, b, "bv_stage")
             at = V_AT + V_COLS * g + V_COLS // 2 * half
             nc.vector.tensor_tensor(
-                out=dst[:, at:at + V_COLS // 2].rearrange("p (n j) -> p n j", j=PACK),
-                in0=v_banks[s, half][:].rearrange("p (j n) -> p n j", j=PACK),
-                in1=bias[:, P * half:P * half + P].unsqueeze(2).to_broadcast([P, P, PACK]),
+                out=dst[:, at + PACK * lo:at + PACK * hi].rearrange("p (n j) -> p n j", j=PACK),
+                in0=v_banks[s, half][:].rearrange("p (j n) -> p n j", j=PACK)[:, lo:hi, :],
+                in1=bias[:, P * half + lo:P * half + hi].unsqueeze(2).to_broadcast([P, hi - lo, PACK]),
                 op=mybir.AluOpType.add,
             )
 
+        v_out = {}
+
         def copy_v_out(s, half):
-            sums = rounds.tile([P, BANK], F32, name="sums")
+            sums = rounds.tile([P, PACK * (P - GP_FROM)], F32, name="sums")
             nc.scalar.copy(
                 out=sums[:].rearrange("p (n j) -> p n j", j=PACK),
-                in_=v_banks[s, half][:].rearrange("p (j n) -> p n j", j=PACK),
+                in_=v_banks[s, half][:].rearrange("p (j n) -> p n j", j=PACK)[:, GP_FROM:P, :],
             )
-            v_banks[s, half] = sums
+            v_out[s] = sums
 
         def add_bias_on_gpsimd(s, half):
             b, g = divmod(s, STEPS_PER_ENTRY)
             dst = stage_of(bv_stage, b, "bv_stage")
-            at = V_AT + V_COLS * g + V_COLS // 2 * half
+            at = V_AT + V_COLS * g + V_COLS // 2 * half + PACK * GP_FROM
             nc.gpsimd.tensor_tensor(
-                out=dst[:, at:at + V_COLS // 2].rearrange("p (n j) -> p n j", j=PACK),
-                in0=v_banks[s, half][:].rearrange("p (n j) -> p n j", j=PACK),
-                in1=bias[:, P * half:P * half + P].unsqueeze(2).to_broadcast([P, P, PACK]),
+                out=dst[:, at:at + PACK * (P - GP_FROM)].rearrange("p (n j) -> p n j", j=PACK),
+                in0=v_out[s][:].rearrange("p (n j) -> p n j", j=PACK),
+                in1=bias[:, P * half + GP_FROM:P * half + P].unsqueeze(2).to_broadcast([P, P - GP_FROM, PACK]),
                 op=mybir.AluOpType.add,
             )
 
         def gate_gpsimd(b):
             gate = rounds.tile([P, 64], U8, name="gate")
-            nc.gpsimd.tensor_copy(out=gate[:], in_=bv_coded[b][1][:, 0:64])
+            nc.gpsimd.tensor_copy(out=gate[:, 0:4], in_=bv_coded[b][1][:, 0:4])
 
         def on_gpsimd(b):
             return 2 <= b < BATCH - 2
@@ -322,8 +325,7 @@ def tile_text2imgca_pb_t_kernel(tc, beta, x2, Wv, bv, out):
                     transpose_beta(b + 1, 0)
                     transpose_beta(b + 1, 1)
                 add_bias(s + 1, 0)
-                if not on_gpsimd(b):
-                    add_bias(s + 1, 1)
+                add_bias(s + 1, 1, 0, GP_FROM if on_gpsimd(b) else P)
                 fp(s + 3)
                 if on_gpsimd(b + 1):
                     copy_v_out(s + 3, 1)

@@ -106,8 +106,8 @@ def tile_text2imgca_pb_t_kernel(tc, beta, x2, Wv, bv, out):
 
         def codes_of(table, b, name):
             if b not in table:
-                codes = rounds.tile([P, K_PASS * STEPS_PER_ENTRY], U32, name=name + "_codes", align_bytes=64)
-                scales = rounds.tile([P, K_PASS * STEPS_PER_ENTRY], U8, name=name + "_scales", align_bytes=64)
+                codes = rounds.tile([P, K_PASS * STEPS_PER_ENTRY], U32, name=name + "_codes", align_bytes=64, bufs=2 if name == "x" else 3)
+                scales = rounds.tile([P, K_PASS * STEPS_PER_ENTRY], U8, name=name + "_scales", align_bytes=64, bufs=2 if name == "x" else 3)
                 table[b] = (codes, scales)
             return table[b]
 
@@ -199,22 +199,25 @@ def tile_text2imgca_pb_t_kernel(tc, beta, x2, Wv, bv, out):
 
         v_out = {}
 
+        def gp_from(s):
+            return 32 if s == STEPS - 2 else GP_FROM
+
         def copy_v_out(s, half):
-            sums = rounds.tile([P, PACK * (P - GP_FROM)], F32, name="sums")
+            sums = rounds.tile([P, PACK * (P - gp_from(s))], F32, name="sums%d" % (s % 2))
             nc.scalar.copy(
                 out=sums[:].rearrange("p (n j) -> p n j", j=PACK),
-                in_=v_banks[s, half][:].rearrange("p (j n) -> p n j", j=PACK)[:, GP_FROM:P, :],
+                in_=v_banks[s, half][:].rearrange("p (j n) -> p n j", j=PACK)[:, gp_from(s):P, :],
             )
             v_out[s] = sums
 
         def add_bias_on_gpsimd(s, half):
             b, g = divmod(s, STEPS_PER_ENTRY)
             dst = stage_of(bv_stage, b, "bv_stage")
-            at = V_AT + V_COLS * g + V_COLS // 2 * half + PACK * GP_FROM
+            at = V_AT + V_COLS * g + V_COLS // 2 * half + PACK * gp_from(s)
             nc.gpsimd.tensor_tensor(
-                out=dst[:, at:at + PACK * (P - GP_FROM)].rearrange("p (n j) -> p n j", j=PACK),
+                out=dst[:, at:at + PACK * (P - gp_from(s))].rearrange("p (n j) -> p n j", j=PACK),
                 in0=v_out[s][:].rearrange("p (n j) -> p n j", j=PACK),
-                in1=bias[:, P * half + GP_FROM:P * half + P].unsqueeze(2).to_broadcast([P, P - GP_FROM, PACK]),
+                in1=bias[:, P * half + gp_from(s):P * half + P].unsqueeze(2).to_broadcast([P, P - gp_from(s), PACK]),
                 op=mybir.AluOpType.add,
             )
 
@@ -312,7 +315,14 @@ def tile_text2imgca_pb_t_kernel(tc, beta, x2, Wv, bv, out):
             if b >= 2 and on_gpsimd(b - 1):
                 gate_gpsimd(b - 2)
                 add_bias_on_gpsimd(s - 1, 1)
-            ab(s)
+            if b + 1 == BATCH:
+                quantise_bv(b - 1)
+                gate_gpsimd(b - 1)
+                add_bias_on_gpsimd(s, 1)
+                add_bias(s, 0)
+                add_bias(s, 1, 0, gp_from(s))
+            else:
+                ab(s)
             if b + 1 < BATCH:
                 quantise_x(s + 2, 2)
                 fp(s + 2)
@@ -329,6 +339,8 @@ def tile_text2imgca_pb_t_kernel(tc, beta, x2, Wv, bv, out):
                 fp(s + 3)
                 if on_gpsimd(b + 1):
                     copy_v_out(s + 3, 1)
+                if b + 2 == BATCH:
+                    copy_v_out(s + 2, 1)
             if b >= 2:
                 second_product(b - 2)
             if b + 3 < BATCH:
@@ -336,7 +348,6 @@ def tile_text2imgca_pb_t_kernel(tc, beta, x2, Wv, bv, out):
                 transpose_x(s + 7, 0)
                 transpose_x(s + 7, 1)
         b = BATCH - 1
-        quantise_bv(b - 1)
         second_product(b - 1)
         ab(STEPS - 1)
         quantise_bv(b, 0, V_AT)

@@ -21,7 +21,7 @@ BETA_COLS = WORDS * PACK
 V_COLS = TEXT * PACK
 V_AT = STEPS_PER_ENTRY * BETA_COLS
 X_SLOTS = 20
-GP_FROM = 64
+GP_FROM = 72
 
 FLOPS = 2 * BATCH * PIXELS * CHANNELS * TEXT + 2 * BATCH * WORDS * PIXELS * TEXT
 
@@ -324,7 +324,7 @@ def tile_text2imgca_pb_t_kernel(tc, beta, x2, Wv, bv, out):
             else:
                 ab(s)
             if b + 1 < BATCH:
-                quantise_x(s + 2, 2)
+                quantise_x(s + 2, 1 if b == 1 else 2)
                 fp(s + 2)
                 if b + 3 <= BATCH:
                     transpose_beta(b, 0)
@@ -336,6 +336,8 @@ def tile_text2imgca_pb_t_kernel(tc, beta, x2, Wv, bv, out):
                     transpose_beta(b + 1, 1)
                 add_bias(s + 1, 0)
                 add_bias(s + 1, 1, 0, GP_FROM if on_gpsimd(b) else P)
+                if b == 1:
+                    quantise_x(s + 3)
                 fp(s + 3)
                 if on_gpsimd(b + 1):
                     copy_v_out(s + 3, 1)

from contextlib import ExitStack

import concourse.masks as masks
import concourse.mybir as mybir

F32 = mybir.dt.float32
BF16 = mybir.dt.bfloat16
U32 = mybir.dt.uint32
U8 = mybir.dt.uint8
FP8X4 = mybir.dt.float8_e4m3fn_x4

P = 128
PACK = 4
BATCH, WORDS, PIXELS, CHANNELS, TEXT = 12, 256, 1024, 512, 256
K_PASS = P * PACK
BANK = 512
STEPS_PER_ENTRY = PIXELS // K_PASS
STEPS = BATCH * STEPS_PER_ENTRY
X_COLS = K_PASS * PACK
BETA_COLS = WORDS * PACK
V_COLS = TEXT * PACK
V_AT = STEPS_PER_ENTRY * BETA_COLS
X_SLOTS = 20
GP_FROM = 72

FLOPS = 2 * BATCH * PIXELS * CHANNELS * TEXT + 2 * BATCH * WORDS * PIXELS * TEXT


def tile_text2imgca_pb_t_kernel(tc, beta, x2, Wv, bv, out):
    nc = tc.nc
    with ExitStack() as ctx:
        keep = ctx.enter_context(tc.tile_pool(name="keep", bufs=1))
        rounds = ctx.enter_context(tc.tile_pool(name="rounds", bufs=2))
        transposed = ctx.enter_context(tc.psum_pool(name="transposed", bufs=4))
        v_sums = ctx.enter_context(tc.psum_pool(name="v_sums", bufs=4))
        ctx.enter_context(tc.manual_schedule())

        x_in = []
        for s in range(X_SLOTS):
            x_t = keep.tile([P, K_PASS * CHANNELS // P], BF16, name="x%d" % s)
            x_in.append(x_t)
        for s in range(X_SLOTS, STEPS):
            x_in.append(x_in[s - X_SLOTS])
        beta_in = []
        for b in range(BATCH):
            beta_t = keep.tile([P, WORDS * PIXELS // P], BF16, name="beta%d" % b)
            beta_in.append(beta_t)
        w_rows = keep.tile([P, PACK * TEXT], BF16, name="w_rows")
        w_stage = keep.tile([P, TEXT * PACK], BF16, name="w_stage", align_bytes=64)
        w_codes = keep.tile([P, TEXT], U32, name="w_codes", align_bytes=64)
        w_scales = keep.tile([P, TEXT], U8, name="w_scales", align_bytes=64)
        bias_row = keep.tile([P, TEXT], BF16, name="bias_row")
        ones = keep.tile([P, P], BF16, name="ones")
        bias = keep.tile([P, TEXT], F32, name="bias")
        identity = keep.tile([P, P], F32, name="identity")

        warm = keep.tile([P, BANK], BF16, name="warm")
        nc.vector.memset(warm[:], 0.0)
        nc.vector.memset(bias_row[:], 0.0)
        nc.vector.memset(ones[:], 1.0)
        masks.make_identity(nc, identity[:])


        def load_x(s):
            b, g = divmod(s, STEPS_PER_ENTRY)
            pixels = x2[b].rearrange("h w c -> (h w) c").rearrange("(g q i) c -> g q (i c)", g=2, q=P, i=4)
            nc.sync.dma_start(out=x_in[s][:], in_=pixels[g])

        def load_beta(b):
            nc.sync.dma_start(out=beta_in[b][:], in_=beta[b].rearrange("(p h) m -> p (h m)", h=2))

        def load_w():
            nc.sync.dma_start(
                out=w_rows[:].rearrange("q (u f) -> q u f", u=2),
                in_=Wv.rearrange("(u q e) n -> q u (e n)", u=2, q=P, e=2),
            )

        load_w()
        load_x(0)
        nc.sync.dma_start(out=bias_row[0:1, :], in_=bv.rearrange("(o n) -> o n", o=1))
        def load_step(s):
            load_x(s)
            if s >= 5 and s % STEPS_PER_ENTRY == 1:
                load_beta((s - 5) // STEPS_PER_ENTRY)

        for s in range(1, X_SLOTS):
            load_step(s)

        nc.vector.tensor_copy(
            out=w_stage[:].rearrange("q (n j) -> q n j", j=PACK),
            in_=w_rows[:].rearrange("q (j n) -> q n j", j=PACK),
        )
        nc.vector.quantize_mx(out=w_codes[:].bitcast(FP8X4), scales=w_scales[:], in_=w_stage[:])

        x_stage = {}
        x_coded = {}
        bv_stage = {}
        bv_coded = {}
        v_banks = {}

        def stage_of(table, b, name):
            if b not in table:
                stage_t = rounds.tile([P, STEPS_PER_ENTRY * X_COLS], BF16, name=name, align_bytes=64, bufs=2 if name == "x_stage" else 3)
                table[b] = stage_t
            return table[b]

        def codes_of(table, b, name):
            if b not in table:
                codes = rounds.tile([P, K_PASS * STEPS_PER_ENTRY], U32, name=name + "_codes", align_bytes=64, bufs=2 if name == "x" else 3)
                scales = rounds.tile([P, K_PASS * STEPS_PER_ENTRY], U8, name=name + "_scales", align_bytes=64, bufs=2 if name == "x" else 3)
                table[b] = (codes, scales)
            return table[b]

        def x_out_of_bank(dst, bank, on_vector=False):
            o = dst.bitcast(F32).rearrange("k (q i u) -> k q i u", i=2, u=2)
            i = bank[:].rearrange("k (i u q) -> k q i u", i=2, u=2)
            if on_vector:
                nc.vector.tensor_copy(out=o, in_=i)
            else:
                nc.scalar.copy(out=o, in_=i)

        def words_out_of_bank(dst, bank, on_vector=False):
            o = dst.bitcast(F32).rearrange("q (i m u) -> q i m u", i=2, u=2)
            i = bank[:].rearrange("q (i u m) -> q i m u", i=2, u=2)
            if on_vector:
                nc.vector.tensor_copy(out=o, in_=i)
            else:
                nc.scalar.copy(out=o, in_=i)

        def transpose_x(s, part=None, on_vector=(False, False)):
            b, g = divmod(s, STEPS_PER_ENTRY)
            words = x_in[s][:].bitcast(F32)
            dst = stage_of(x_stage, b, "x_stage")
            for half in range(2) if part is None else [part]:
                bank = transposed.tile([P, BANK], F32, name="tr")
                for i in range(2):
                    for u in range(2):
                        at = 2 * P * (half + 2 * i) + P * u
                        to = P * (2 * i + u)
                        nc.tensor.transpose(bank[:, to:to + P], words[:, at:at + P], identity[:])
                to = X_COLS * g + X_COLS // 2 * half
                x_out_of_bank(dst[:, to:to + X_COLS // 2], bank, on_vector[half])

        def transpose_beta(b, part=None):
            words = beta_in[b][:].bitcast(F32)
            dst = stage_of(bv_stage, b, "bv_stage")
            for g in range(STEPS_PER_ENTRY) if part is None else [part]:
                bank = transposed.tile([P, BANK], F32, name="tr")
                for h in range(2):
                    for u in range(2):
                        at = PIXELS // 2 * h + P * (2 * g + u)
                        to = P * (2 * h + u)
                        nc.tensor.transpose(bank[:, to:to + P], words[:, at:at + P], identity[:])
                words_out_of_bank(dst[:, BETA_COLS * g:BETA_COLS * (g + 1)], bank)

        def quantise(table, coded, b, name, lo, hi):
            codes, scales = codes_of(coded, b, name)
            nc.vector.quantize_mx(
                out=codes[:, lo // PACK:hi // PACK].bitcast(FP8X4),
                scales=scales[:, lo // PACK:hi // PACK],
                in_=table[b][:, lo:hi],
            )

        def quantise_x(s, steps=1):
            b, g = divmod(s, STEPS_PER_ENTRY)
            quantise(x_stage, x_coded, b, "x", X_COLS * g, X_COLS * (g + steps))

        def quantise_bv(b, lo=0, hi=STEPS_PER_ENTRY * X_COLS):
            quantise(bv_stage, bv_coded, b, "bv", lo, hi)

        def first_product(s, half):
            b, g = divmod(s, STEPS_PER_ENTRY)
            codes, scales = x_coded[b]
            bank = v_sums.tile([P, BANK], F32, name="v")
            for t in range(PACK):
                at = K_PASS * g + P * t
                j = 2 * (t % 2) + t // 2
                nc.tensor.matmul_mx(
                    out=bank[:, P * j:P * j + P],
                    lhsT=codes[:, at:at + P].bitcast(FP8X4),
                    lhsT_scale=scales[:, at:at + P],
                    rhs=w_codes[:, P * half:P * half + P].bitcast(FP8X4),
                    rhs_scale=w_scales[:, P * half:P * half + P],
                    start=True,
                    stop=True,
                )
            v_banks[s, half] = bank

        def add_bias(s, half, lo=0, hi=P):
            b, g = divmod(s, STEPS_PER_ENTRY)
            dst = stage_of(bv_stage, b, "bv_stage")
            at = V_AT + V_COLS * g + V_COLS // 2 * half
            nc.vector.tensor_tensor(
                out=dst[:, at + PACK * lo:at + PACK * hi].rearrange("p (n j) -> p n j", j=PACK),
                in0=v_banks[s, half][:].rearrange("p (j n) -> p n j", j=PACK)[:, lo:hi, :],
                in1=bias[:, P * half + lo:P * half + hi].unsqueeze(2).to_broadcast([P, hi - lo, PACK]),
                op=mybir.AluOpType.add,
            )

        v_out = {}

        def gp_from(s):
            return 32 if s == STEPS - 2 else GP_FROM

        def copy_v_out(s, half):
            sums = rounds.tile([P, PACK * (P - gp_from(s))], F32, name="sums%d" % (s % 2))
            nc.scalar.copy(
                out=sums[:].rearrange("p (n j) -> p n j", j=PACK),
                in_=v_banks[s, half][:].rearrange("p (j n) -> p n j", j=PACK)[:, gp_from(s):P, :],
            )
            v_out[s] = sums

        def add_bias_on_gpsimd(s, half):
            b, g = divmod(s, STEPS_PER_ENTRY)
            dst = stage_of(bv_stage, b, "bv_stage")
            at = V_AT + V_COLS * g + V_COLS // 2 * half + PACK * gp_from(s)
            nc.gpsimd.tensor_tensor(
                out=dst[:, at:at + PACK * (P - gp_from(s))].rearrange("p (n j) -> p n j", j=PACK),
                in0=v_out[s][:].rearrange("p (n j) -> p n j", j=PACK),
                in1=bias[:, P * half + gp_from(s):P * half + P].unsqueeze(2).to_broadcast([P, P - gp_from(s), PACK]),
                op=mybir.AluOpType.add,
            )

        def gate_gpsimd(b):
            gate = rounds.tile([P, 64], U8, name="gate")
            nc.gpsimd.tensor_copy(out=gate[:, 0:4], in_=bv_coded[b][1][:, 0:4])

        def on_gpsimd(b):
            return 2 <= b < BATCH - 2

        def second_pass(sums, b, g, h):
            codes, scales = bv_coded[b]
            beta_at = (BETA_COLS * g) // PACK + P * h
            v_at = (V_AT + V_COLS * g) // PACK
            nc.tensor.matmul_mx(
                out=sums,
                lhsT=codes[:, beta_at:beta_at + P].bitcast(FP8X4),
                lhsT_scale=scales[:, beta_at:beta_at + P],
                rhs=codes[:, v_at:v_at + TEXT].bitcast(FP8X4),
                rhs_scale=scales[:, v_at:v_at + TEXT],
                start=(g == 0),
                stop=(g == STEPS_PER_ENTRY - 1),
            )

        def second_product(b):
            bank = transposed.tile([P, BANK], F32, name="tr")
            for h in range(2):
                for g in range(STEPS_PER_ENTRY):
                    second_pass(bank[:, TEXT * h:TEXT * h + TEXT], b, g, h)
            result = keep.tile([P, 2 * TEXT], F32, name="out%d" % b)
            nc.scalar.copy(out=result[:], in_=bank[:])
            nc.sync.dma_start(out=out[b].rearrange("(p h) n -> p (h n)", h=2), in_=result[:])

        last_banks = []

        def last_product(g):
            b = BATCH - 1
            if g == 0:
                bank0 = transposed.tile([P, BANK], F32, name="tr")
                bank1 = transposed.tile([P, BANK], F32, name="tr")
                last_banks.append(bank0)
                last_banks.append(bank1)
            for h in range(2):
                second_pass(last_banks[h][:, 0:TEXT], b, g, h)
            if g == STEPS_PER_ENTRY - 1:
                rows = out[b].rearrange("(p h) n -> p h n", h=2)
                result0 = keep.tile([P, TEXT], F32, name="out_last0")
                result1 = keep.tile([P, TEXT], F32, name="out_last1")
                nc.scalar.copy(out=result0[:], in_=last_banks[0][:, 0:TEXT])
                nc.sync.dma_start(out=rows[:, 0, :], in_=result0[:])
                nc.vector.tensor_copy(out=result1[:], in_=last_banks[1][:, 0:TEXT])
                nc.sync.dma_start(out=rows[:, 1, :], in_=result1[:])

        bank = transposed.tile([P, BANK], F32, name="tr")
        for i in range(7):
            nc.tensor.matmul(out=bank[:], lhsT=warm[:, 0:P], rhs=warm[:], start=True, stop=True)
        def fp(s):
            first_product(s, 0)
            first_product(s, 1)

        def ab(s):
            add_bias(s, 0)
            add_bias(s, 1)

        transpose_x(0, None, (False, True))
        bank = transposed.tile([P, BANK], F32, name="tr")
        nc.tensor.matmul(out=bank[:, 0:TEXT], lhsT=ones[:], rhs=bias_row[:], start=True, stop=True)
        nc.scalar.copy(out=bias[:], in_=bank[:, 0:TEXT])
        quantise_x(0)
        transpose_x(1, None, (False, True))
        transpose_x(2)
        fp(0)
        quantise_x(1)
        transpose_x(3)
        fp(1)
        ab(0)
        quantise_x(2)
        transpose_x(4)
        fp(2)
        ab(1)
        quantise_x(3)
        transpose_x(5)
        fp(3)
        for s in range(X_SLOTS, STEPS):
            load_step(s)
        load_beta(BATCH - 2)
        load_beta(BATCH - 1)
        transpose_beta(0)
        transpose_x(6)
        transpose_x(7)
        for b in range(1, BATCH):
            s = STEPS_PER_ENTRY * b
            if b >= 2:
                quantise_bv(b - 2)
            if b >= 2 and on_gpsimd(b - 1):
                gate_gpsimd(b - 2)
                add_bias_on_gpsimd(s - 1, 1)
            if b + 1 == BATCH:
                quantise_bv(b - 1)
                gate_gpsimd(b - 1)
                add_bias_on_gpsimd(s, 1)
                add_bias(s, 0)
                add_bias(s, 1, 0, gp_from(s))
            else:
                ab(s)
            if b + 1 < BATCH:
                quantise_x(s + 2, 1 if b == 1 else 2)
                fp(s + 2)
                if b + 3 <= BATCH:
                    transpose_beta(b, 0)
                    transpose_beta(b, 1)
                if b + 3 < BATCH:
                    transpose_x(s + 6, 0)
                elif b + 1 < BATCH:
                    transpose_beta(b + 1, 0)
                    transpose_beta(b + 1, 1)
                add_bias(s + 1, 0)
                add_bias(s + 1, 1, 0, GP_FROM if on_gpsimd(b) else P)
                if b == 1:
                    quantise_x(s + 3)
                fp(s + 3)
                if on_gpsimd(b + 1):
                    copy_v_out(s + 3, 1)
                if b + 2 == BATCH:
                    copy_v_out(s + 2, 1)
            if b >= 2:
                second_product(b - 2)
            if b + 3 < BATCH:
                transpose_x(s + 6, 1)
                transpose_x(s + 7, 0)
                transpose_x(s + 7, 1)
        b = BATCH - 1
        second_product(b - 1)
        ab(STEPS - 1)
        quantise_bv(b, 0, V_AT)
        quantise_bv(b, V_AT, V_AT + V_COLS)
        last_product(0)
        quantise_bv(b, V_AT + V_COLS, V_AT + 2 * V_COLS)
        last_product(1)
